import numpy as np
import ml_dtypes


def mxq(x, axis, fmt="e4m3"):
    dtype, down = {"e4m3": (ml_dtypes.float8_e4m3fn, 7), "e5m2": (ml_dtypes.float8_e5m2, 14)}[fmt]
    v = np.moveaxis(np.asarray(x, np.float32).astype(ml_dtypes.bfloat16).astype(np.float64), axis, -1)
    blocks = v.reshape(v.shape[:-1] + (-1, 32))
    amax = np.abs(blocks).max(-1, keepdims=True)
    byte = np.maximum(np.where(amax > 0, np.frexp(amax)[1] - 1 + 127, 0) - down, 1)
    scale = np.exp2(byte - 127.0)
    codes = (blocks / scale).astype(np.float32).astype(dtype).astype(np.float64)
    return np.moveaxis((codes * scale).reshape(v.shape), -1, axis)


WIDE = False


def mx_kscale(k):
    if not WIDE:
        return np.ones(k)
    levels = np.array([10, -10, 5, -5, 0])
    a = np.random.permutation(np.resize(levels, k // 512 * 4)).reshape(k // 512, 4)
    idx = np.arange(k)
    return np.exp2(a[idx // 512, idx % 128 // 32])


BF16 = ml_dtypes.bfloat16


def bf(x):
    return np.asarray(x, np.float32).astype(BF16)


def f64(x):
    return np.asarray(x).astype(np.float64)


B, I, H = 4096, 256, 512


def sigmoid(v):
    return 1.0 / (1.0 + np.exp(-v))


def setup_inputs():
    s = mx_kscale(H)
    return {"x_t": bf(np.random.standard_normal((B, I))),
            "h": bf(np.random.standard_normal((B, H)) * s),
            "c": bf(np.random.standard_normal((B, H))),
            "W_ih": bf(np.random.standard_normal((4 * H, I)) * 0.7 / np.sqrt(I)),
            "W_hh": bf(np.random.standard_normal((4 * H, H)) * 0.7 / np.sqrt(H) / s),
            "b_ih": bf(np.random.standard_normal(4 * H) * 0.3),
            "b_hh": bf(np.random.standard_normal(4 * H) * 0.3)}


def reference(x_t, h, c, W_ih, W_hh, b_ih, b_hh):
    gates = f64(x_t) @ f64(W_ih).T + f64(b_ih) + (mxq(f64(h), 1, "e4m3") @ mxq(f64(W_hh), 1, "e4m3").T) + f64(b_hh)
    i, f, g, o = np.split(gates, 4, axis=1)
    c_next = sigmoid(f) * f64(c) + sigmoid(i) * np.tanh(g)
    h_next = sigmoid(o) * np.tanh(c_next)
    return h_next, c_next

@@ -1,0 +1,308 @@
+from contextlib import ExitStack
+
+import concourse.mybir as mybir
+from concourse.masks import make_identity
+
+F32 = mybir.dt.float32
+BF16 = mybir.dt.bfloat16
+U32 = mybir.dt.uint32
+U8 = mybir.dt.uint8
+FP8X4 = mybir.dt.float8_e4m3fn_x4
+ACT = mybir.ActivationFunctionType
+ALU = mybir.AluOpType
+
+P = 128
+BATCH, IN_DIM, HID = 4096, 256, 512
+GATES = 4
+GATE_I, GATE_F, GATE_G, GATE_O = 0, 1, 2, 3
+TILES = 4
+GROUP_ROWS = TILES * P
+N_GROUPS = BATCH // GROUP_ROWS
+N_TILES = N_GROUPS * TILES
+N_STEPS = N_TILES * GATES
+BLOCKS_PER_GATE = HID // P
+BLOCKS = GATES * BLOCKS_PER_GATE
+X_PASSES = IN_DIM // P
+WORD_HALVES = 2
+PACK = 4
+
+KEEP_LAG = GATE_F + 1
+WRITE_LAG = GATE_G + 1
+CELL_LAG = WRITE_LAG + 2
+TANH_LAG = CELL_LAG + 1
+HIDDEN_LAG = TANH_LAG + 1
+
+FLOPS = 2 * BATCH * GATES * HID * (IN_DIM + HID)
+
+
+def tile_nodelstmcell_pa_t_kernel(tc, x_t, h, c, W_ih, W_hh, b_ih, b_hh, out_0, out_1):
+    nc = tc.nc
+
+    x_rows = x_t.rearrange("(s p j) k -> s p (j k)", p=P, j=TILES)
+    h_rows = h.rearrange("(s p j) k -> s p (j k)", p=P, j=TILES)
+    c_rows = c.rearrange("(s p j) n -> s p (j n)", p=P, j=TILES)
+    h_next_rows = out_0.rearrange("(s p j) n -> s p (j n)", p=P, j=TILES)
+    c_next_rows = out_1.rearrange("(s p j) n -> s p (j n)", p=P, j=TILES)
+
+    with ExitStack() as stack:
+        const = stack.enter_context(tc.tile_pool(name="const", bufs=1))
+        setup = stack.enter_context(tc.tile_pool(name="setup", bufs=4))
+        rows = stack.enter_context(tc.tile_pool(name="rows", bufs=3))
+        operands = stack.enter_context(tc.tile_pool(name="operands", bufs=2))
+        work = stack.enter_context(tc.tile_pool(name="work", bufs=2))
+        psum = stack.enter_context(tc.psum_pool(name="psum", bufs=1))
+        stack.enter_context(tc.manual_schedule())
+
+        x_in, h_in, c_in = {}, {}, {}
+        x_T, h_codes, h_scales = {}, {}, {}
+        rec_T = {}
+        gate_ps = {}
+        acts = {}
+        tanh_c = {}
+        c_new, h_new = {}, {}
+
+        def load_rows(s):
+            h_in[s] = rows.tile([P, TILES * HID], BF16, name="h_in", tag="h_in")
+            nc.sync.dma_start(out=h_in[s][:], in_=h_rows[s])
+            x_in[s] = rows.tile([P, TILES * IN_DIM], BF16, name="x_in", tag="x_in")
+            nc.sync.dma_start(out=x_in[s][:], in_=x_rows[s])
+
+        def load_cell(s):
+            c_in[s] = rows.tile([P, TILES * HID], BF16, name="c_in", tag="c_in")
+            nc.sync.dma_start(out=c_in[s][:], in_=c_rows[s])
+
+        def transpose_rows(s, j):
+            if j == 0:
+                h_codes[s] = operands.tile([P, GROUP_ROWS], U32, name="h_codes", tag="h_codes", align_bytes=64)
+                h_scales[s] = operands.tile([P, GROUP_ROWS], U8, name="h_scales", tag="h_scales", align_bytes=64)
+                x_T[s] = operands.tile([P, TILES, X_PASSES, P], BF16, name="x_T", tag="x_T", bufs=3)
+            h_words = h_in[s][:].bitcast(F32)
+            hT_ps = psum.tile([P, WORD_HALVES, P], F32, tag="hT")
+            for u in range(WORD_HALVES):
+                first = (j * WORD_HALVES + u) * P
+                nc.tensor.transpose(hT_ps[:, u, :], h_words[:, first : first + P], ident_f32[:])
+            h_grouped = work.tile([P, P * PACK], BF16, tag="h_grouped", align_bytes=64)
+            nc.scalar.copy(
+                out=h_grouped[:].bitcast(F32).rearrange("p (r u) -> p r u", u=WORD_HALVES),
+                in_=hT_ps[:].rearrange("p u r -> p r u"),
+            )
+            xT_ps = psum.tile([P, X_PASSES, P], BF16, tag="xT")
+            for kc in range(X_PASSES):
+                first = j * IN_DIM + kc * P
+                nc.tensor.transpose(xT_ps[:, kc, :], x_in[s][:, first : first + P], ident_bf16[:])
+            nc.scalar.copy(out=x_T[s][:, j, :, :], in_=xT_ps[:])
+            return h_grouped
+
+        def quantise_rows(s, j, h_grouped):
+            cols = slice(j * P, (j + 1) * P)
+            nc.vector.quantize_mx(
+                out=h_codes[s][:, cols].bitcast(FP8X4), scales=h_scales[s][:, cols], in_=h_grouped[:]
+            )
+
+        def recurrent_block(s, blk):
+            if blk == 0:
+                rec_T[s] = operands.tile([P, BLOCKS, GROUP_ROWS], F32, name="rec_T", tag="rec_T")
+            cols = slice(blk * P, (blk + 1) * P)
+            rec_ps = psum.tile([P, GROUP_ROWS], F32, tag="rec", bufs=2)
+            nc.tensor.matmul_mx(
+                out=rec_ps[:],
+                lhsT=w_codes[:, cols].bitcast(FP8X4),
+                lhsT_scale=w_scales[:, cols],
+                rhs=h_codes[s][:].bitcast(FP8X4),
+                rhs_scale=h_scales[s][:],
+                start=True,
+                stop=True,
+            )
+            nc.vector.tensor_scalar(
+                out=rec_T[s][:, blk, :], in0=rec_ps[:], scalar1=bias[:, blk : blk + 1], scalar2=None, op0=ALU.add
+            )
+
+        def input_pass(step, kc):
+            tile_index, gate = divmod(step, GATES)
+            s, j = divmod(tile_index, TILES)
+            if kc == 0:
+                gate_ps[step] = psum.tile([P, HID], F32, name="gate_ps", tag="gate", bufs=4)
+            nc.tensor.matmul(
+                out=gate_ps[step][:],
+                lhsT=x_T[s][:, j, kc, :],
+                rhs=w_ih_T[:, kc, gate * HID : (gate + 1) * HID],
+                start=(kc == 0),
+                stop=False,
+            )
+
+        def add_recurrent_and_activate(step):
+            tile_index, gate = divmod(step, GATES)
+            s, j = divmod(tile_index, TILES)
+            for a in range(BLOCKS_PER_GATE):
+                nc.tensor.matmul(
+                    out=gate_ps[step][:, a * P : (a + 1) * P],
+                    lhsT=rec_T[s][:, gate * BLOCKS_PER_GATE + a, j * P : (j + 1) * P],
+                    rhs=ident_f32[:],
+                    is_transpose=True,
+                    start=False,
+                    stop=(a == BLOCKS_PER_GATE - 1),
+                )
+            acts[tile_index, gate] = work.tile([P, HID], F32, name="act%d" % gate, tag="act%d" % gate)
+            nc.scalar.activation(
+                out=acts[tile_index, gate][:],
+                in_=gate_ps[step][:],
+                func=(ACT.Tanh if gate == GATE_G else ACT.Sigmoid),
+            )
+
+        def keep_old_cell(tile_index):
+            s, j = divmod(tile_index, TILES)
+            keep = acts[tile_index, GATE_F]
+            nc.gpsimd.tensor_tensor(out=keep[:], in0=keep[:], in1=c_in[s][:, j * HID : (j + 1) * HID], op=ALU.mult)
+
+        def write_candidate(tile_index):
+            write = acts[tile_index, GATE_I]
+            nc.gpsimd.tensor_tensor(out=write[:], in0=write[:], in1=acts[tile_index, GATE_G][:], op=ALU.mult)
+
+        def new_cell(tile_index):
+            s, j = divmod(tile_index, TILES)
+            if j == 0:
+                c_new[s] = work.tile([P, TILES * HID], F32, name="c_new", tag="c_new")
+            nc.vector.tensor_tensor(
+                out=c_new[s][:, j * HID : (j + 1) * HID],
+                in0=acts[tile_index, GATE_F][:],
+                in1=acts[tile_index, GATE_I][:],
+                op=ALU.add,
+            )
+            if j == TILES - 1:
+                nc.sync.dma_start(out=c_next_rows[s], in_=c_new[s][:])
+
+        def tanh_of_new_cell(tile_index):
+            s, j = divmod(tile_index, TILES)
+            tanh_c[tile_index] = work.tile([P, HID], F32, name="tanh_c", tag="tanh_c")
+            nc.scalar.activation(out=tanh_c[tile_index][:], in_=c_new[s][:, j * HID : (j + 1) * HID], func=ACT.Tanh)
+
+        def new_hidden(tile_index):
+            s, j = divmod(tile_index, TILES)
+            if j == 0:
+                h_new[s] = work.tile([P, TILES * HID], F32, name="h_new", tag="h_new")
+            nc.vector.tensor_tensor(
+                out=h_new[s][:, j * HID : (j + 1) * HID],
+                in0=acts[tile_index, GATE_O][:],
+                in1=tanh_c[tile_index][:],
+                op=ALU.mult,
+            )
+            if j == TILES - 1:
+                nc.sync.dma_start(out=h_next_rows[s], in_=h_new[s][:])
+
+        def tile_due(step, lag):
+            tile_index, rest = divmod(step - lag, GATES)
+            return tile_index if rest == 0 and 0 <= tile_index < N_TILES else None
+
+        bias_rows = const.tile([P, P], BF16)
+        nc.vector.memset(bias_rows[:], 0.0)
+        nc.sync.dma_start(out=bias_rows[0:BLOCKS, :], in_=b_ih.rearrange("(b n) -> b n", n=P))
+        nc.sync.dma_start(out=bias_rows[BLOCKS : 2 * BLOCKS, :], in_=b_hh.rearrange("(b n) -> b n", n=P))
+        load_rows(0)
+        w_hh_raw, w_ih_raw = [], []
+        for gate in range(GATES):
+            raw = setup.tile([P, BLOCKS_PER_GATE, HID], BF16, name="w_hh_raw", tag="w_hh_raw")
+            nc.sync.dma_start(
+                out=raw[:], in_=W_hh[gate * HID : (gate + 1) * HID, :].rearrange("(a p) k -> p a k", p=P)
+            )
+            w_hh_raw.append(raw)
+        for gate in range(GATES):
+            raw = setup.tile([P, BLOCKS_PER_GATE, IN_DIM], BF16, name="w_ih_raw", tag="w_ih_raw")
+            nc.sync.dma_start(
+                out=raw[:], in_=W_ih[gate * HID : (gate + 1) * HID, :].rearrange("(a p) k -> p a k", p=P)
+            )
+            w_ih_raw.append(raw)
+        load_rows(1)
+        load_cell(0)
+        load_rows(2)
+
+        ident_f32 = const.tile([P, P], F32)
+        make_identity(nc, ident_f32[:])
+        ident_bf16 = const.tile([P, P], BF16)
+        make_identity(nc, ident_bf16[:])
+
+        biasT_ps = psum.tile([P, P], BF16, tag="xT")
+        nc.tensor.transpose(biasT_ps[:], bias_rows[:], ident_bf16[:])
+        bias_pair = const.tile([P, 2 * BLOCKS], F32)
+        nc.vector.tensor_copy(out=bias_pair[:], in_=biasT_ps[:, 0 : 2 * BLOCKS])
+        bias = const.tile([P, BLOCKS], F32)
+        nc.vector.tensor_tensor(out=bias[:], in0=bias_pair[:, 0:BLOCKS], in1=bias_pair[:, BLOCKS : 2 * BLOCKS], op=ALU.add)
+
+        for j in range(TILES):
+            quantise_rows(0, j, transpose_rows(0, j))
+
+        w_codes = const.tile([P, GATES * HID], U32, align_bytes=64)
+        w_scales = const.tile([P, GATES * HID], U8, align_bytes=64)
+        for gate in range(GATES):
+            w_grouped = setup.tile([P, HID * PACK], BF16, tag="w_grouped", bufs=2, align_bytes=64)
+            grouped_words = w_grouped[:].bitcast(F32).rearrange(
+                "p (a n u) -> p a n u", a=BLOCKS_PER_GATE, u=WORD_HALVES
+            )
+            for half in range(2):
+                wT_ps = psum.tile([P, 2, WORD_HALVES, P], F32, tag="gate", bufs=4)
+                for a in range(2):
+                    raw_words = w_hh_raw[gate][:, 2 * half + a, :].bitcast(F32)
+                    for u in range(WORD_HALVES):
+                        nc.tensor.transpose(wT_ps[:, a, u, :], raw_words[:, u * P : (u + 1) * P], ident_f32[:])
+                nc.scalar.copy(
+                    out=grouped_words[:, 2 * half : 2 * half + 2, :, :], in_=wT_ps[:].rearrange("p a u n -> p a n u")
+                )
+            cols = slice(gate * HID, (gate + 1) * HID)
+            nc.vector.quantize_mx(out=w_codes[:, cols].bitcast(FP8X4), scales=w_scales[:, cols], in_=w_grouped[:])
+            for a in range(BLOCKS_PER_GATE):
+                recurrent_block(0, gate * BLOCKS_PER_GATE + a)
+
+        w_ih_T = const.tile([P, X_PASSES, GATES * HID], BF16)
+        for gate in range(GATES):
+            wT_ps = psum.tile([P, X_PASSES, BLOCKS_PER_GATE, P], BF16, tag="gate", bufs=4)
+            for a in range(BLOCKS_PER_GATE):
+                for kc in range(X_PASSES):
+                    nc.tensor.transpose(wT_ps[:, kc, a, :], w_ih_raw[gate][:, a, kc * P : (kc + 1) * P], ident_bf16[:])
+            nc.scalar.copy(
+                out=w_ih_T[:, :, gate * HID : (gate + 1) * HID], in_=wT_ps[:].rearrange("p kc a n -> p kc (a n)")
+            )
+
+        for j in range(TILES):
+            quantise_rows(1, j, transpose_rows(1, j))
+
+        grouped_waiting = {}
+        for step in range(N_STEPS + HIDDEN_LAG):
+            tile_index, gate = divmod(step, GATES)
+            s, j = divmod(tile_index, TILES)
+            running = step < N_STEPS
+
+            if running and gate == 0 and j == 0:
+                if s + 3 < N_GROUPS:
+                    load_rows(s + 3)
+                if s + 1 < N_GROUPS:
+                    load_cell(s + 1)
+
+            if running:
+                input_pass(step, 0)
+            if 0 < step <= N_STEPS:
+                add_recurrent_and_activate(step - 1)
+
+            due = tile_due(step, KEEP_LAG)
+            if due is not None:
+                keep_old_cell(due)
+            due = tile_due(step, WRITE_LAG)
+            if due is not None:
+                write_candidate(due)
+            due = tile_due(step, CELL_LAG)
+            if due is not None:
+                new_cell(due)
+            due = tile_due(step, TANH_LAG)
+            if due is not None:
+                tanh_of_new_cell(due)
+            due = tile_due(step, HIDDEN_LAG)
+            if due is not None:
+                new_hidden(due)
+
+            if running and s + 2 < N_GROUPS:
+                if gate == 0:
+                    grouped_waiting[j] = transpose_rows(s + 2, j)
+                if gate == 1:
+                    quantise_rows(s + 2, j, grouped_waiting[j])
+            if running:
+                input_pass(step, 1)
+            if running and s + 1 < N_GROUPS:
+                recurrent_block(s + 1, j * GATES + gate)

@@ -26,11 +26,14 @@ X_PASSES = IN_DIM // P
 WORD_HALVES = 2
 PACK = 4
 
+VECTOR_JOINED = (GATE_I, GATE_F)
+TENSOR_JOINED = (GATE_G, GATE_O)
+
 KEEP_LAG = GATE_F + 1
 WRITE_LAG = GATE_G + 1
-CELL_LAG = WRITE_LAG + 2
+CELL_LAG = GATES + GATE_F
 TANH_LAG = CELL_LAG + 1
-HIDDEN_LAG = TANH_LAG + 1
+HIDDEN_LAG = 2 * GATES + GATE_I
 
 FLOPS = 2 * BATCH * GATES * HID * (IN_DIM + HID)
 
@@ -49,7 +52,8 @@ def tile_nodelstmcell_pa_t_kernel(tc, x_t, h, c, W_ih, W_hh, b_ih, b_hh, out_0, 
         setup = stack.enter_context(tc.tile_pool(name="setup", bufs=4))
         rows = stack.enter_context(tc.tile_pool(name="rows", bufs=3))
         operands = stack.enter_context(tc.tile_pool(name="operands", bufs=2))
-        work = stack.enter_context(tc.tile_pool(name="work", bufs=2))
+        work = stack.enter_context(tc.tile_pool(name="work", bufs=3))
+        results = stack.enter_context(tc.tile_pool(name="results", bufs=2))
         psum = stack.enter_context(tc.psum_pool(name="psum", bufs=1))
         stack.enter_context(tc.manual_schedule())
 
@@ -57,9 +61,15 @@ def tile_nodelstmcell_pa_t_kernel(tc, x_t, h, c, W_ih, W_hh, b_ih, b_hh, out_0, 
         x_T, h_codes, h_scales = {}, {}, {}
         rec_T = {}
         gate_ps = {}
+        rec_ps = {}
         acts = {}
         tanh_c = {}
         c_new, h_new = {}, {}
+
+        def place(step):
+            tile_index, gate = divmod(step, GATES)
+            s, j = divmod(tile_index, TILES)
+            return tile_index, gate, s, j
 
         def load_rows(s):
             h_in[s] = rows.tile([P, TILES * HID], BF16, name="h_in", tag="h_in")
@@ -73,8 +83,8 @@ def tile_nodelstmcell_pa_t_kernel(tc, x_t, h, c, W_ih, W_hh, b_ih, b_hh, out_0, 
 
         def transpose_rows(s, j):
             if j == 0:
-                h_codes[s] = operands.tile([P, GROUP_ROWS], U32, name="h_codes", tag="h_codes", align_bytes=64)
-                h_scales[s] = operands.tile([P, GROUP_ROWS], U8, name="h_scales", tag="h_scales", align_bytes=64)
+                h_codes[s] = operands.tile([P, GROUP_ROWS], U32, name="h_codes", tag="h_codes", bufs=3, align_bytes=64)
+                h_scales[s] = operands.tile([P, GROUP_ROWS], U8, name="h_scales", tag="h_scales", bufs=3, align_bytes=64)
                 x_T[s] = operands.tile([P, TILES, X_PASSES, P], BF16, name="x_T", tag="x_T", bufs=3)
             h_words = h_in[s][:].bitcast(F32)
             hT_ps = psum.tile([P, WORD_HALVES, P], F32, tag="hT")
@@ -99,13 +109,55 @@ def tile_nodelstmcell_pa_t_kernel(tc, x_t, h, c, W_ih, W_hh, b_ih, b_hh, out_0, 
                 out=h_codes[s][:, cols].bitcast(FP8X4), scales=h_scales[s][:, cols], in_=h_grouped[:]
             )
 
-        def recurrent_block(s, blk):
-            if blk == 0:
-                rec_T[s] = operands.tile([P, BLOCKS, GROUP_ROWS], F32, name="rec_T", tag="rec_T")
-            cols = slice(blk * P, (blk + 1) * P)
-            rec_ps = psum.tile([P, GROUP_ROWS], F32, tag="rec", bufs=2)
+        def input_pass(step, kc):
+            tile_index, gate, s, j = place(step)
+            if kc == 0:
+                gate_ps[step] = psum.tile([P, HID], F32, name="gate_ps", tag="gate", bufs=3)
+            nc.tensor.matmul(
+                out=gate_ps[step][:],
+                lhsT=x_T[s][:, j, kc, :],
+                rhs=w_ih_T[:, kc, gate * HID : (gate + 1) * HID],
+                start=(kc == 0),
+                stop=(kc == X_PASSES - 1 and gate in VECTOR_JOINED),
+            )
+
+        def add_bias(step):
+            tile_index, gate, s, j = place(step)
+            acts[tile_index, gate] = work.tile([P, HID], F32, name="act%d" % gate, tag="act%d" % gate)
+            spread = VECTOR_JOINED.index(gate) * HID
+            nc.vector.tensor_tensor(
+                out=acts[tile_index, gate][:], in0=gate_ps[step][:], in1=bias_spread[:, spread : spread + HID], op=ALU.add
+            )
+
+        def recurrent_rows(step):
+            tile_index, gate, s, j = place(step)
+            rec_ps[step] = psum.tile([P, HID], F32, name="rec_ps", tag="rec", bufs=3)
             nc.tensor.matmul_mx(
-                out=rec_ps[:],
+                out=rec_ps[step][:],
+                lhsT=h_codes[s][:, j * P : (j + 1) * P].bitcast(FP8X4),
+                lhsT_scale=h_scales[s][:, j * P : (j + 1) * P],
+                rhs=w_codes[:, gate * HID : (gate + 1) * HID].bitcast(FP8X4),
+                rhs_scale=w_scales[:, gate * HID : (gate + 1) * HID],
+                start=True,
+                stop=True,
+            )
+
+        def join_and_activate(step):
+            tile_index, gate, s, j = place(step)
+            total = acts[tile_index, gate]
+            nc.vector.tensor_tensor(out=total[:], in0=rec_ps[step][:], in1=total[:], op=ALU.add)
+            nc.scalar.activation(out=total[:], in_=total[:], func=(ACT.Tanh if gate == GATE_G else ACT.Sigmoid))
+
+        def recurrent_block(s, local):
+            if local == 0:
+                rec_T[s] = operands.tile(
+                    [P, len(TENSOR_JOINED) * BLOCKS_PER_GATE, GROUP_ROWS], F32, name="rec_T", tag="rec_T"
+                )
+            blk = TENSOR_JOINED[local // BLOCKS_PER_GATE] * BLOCKS_PER_GATE + local % BLOCKS_PER_GATE
+            cols = slice(blk * P, (blk + 1) * P)
+            recT_ps = psum.tile([P, GROUP_ROWS], F32, tag="rec", bufs=3)
+            nc.tensor.matmul_mx(
+                out=recT_ps[:],
                 lhsT=w_codes[:, cols].bitcast(FP8X4),
                 lhsT_scale=w_scales[:, cols],
                 rhs=h_codes[s][:].bitcast(FP8X4),
@@ -113,30 +165,21 @@ def tile_nodelstmcell_pa_t_kernel(tc, x_t, h, c, W_ih, W_hh, b_ih, b_hh, out_0, 
                 start=True,
                 stop=True,
             )
-            nc.vector.tensor_scalar(
-                out=rec_T[s][:, blk, :], in0=rec_ps[:], scalar1=bias[:, blk : blk + 1], scalar2=None, op0=ALU.add
-            )
-
-        def input_pass(step, kc):
-            tile_index, gate = divmod(step, GATES)
-            s, j = divmod(tile_index, TILES)
-            if kc == 0:
-                gate_ps[step] = psum.tile([P, HID], F32, name="gate_ps", tag="gate", bufs=4)
-            nc.tensor.matmul(
-                out=gate_ps[step][:],
-                lhsT=x_T[s][:, j, kc, :],
-                rhs=w_ih_T[:, kc, gate * HID : (gate + 1) * HID],
-                start=(kc == 0),
-                stop=False,
-            )
+            if local % 2 == 0:
+                nc.scalar.activation(
+                    out=rec_T[s][:, local, :], in_=recT_ps[:], func=ACT.Identity, bias=bias[:, blk : blk + 1]
+                )
+            else:
+                nc.vector.tensor_scalar(
+                    out=rec_T[s][:, local, :], in0=recT_ps[:], scalar1=bias[:, blk : blk + 1], scalar2=None, op0=ALU.add
+                )
 
         def add_recurrent_and_activate(step):
-            tile_index, gate = divmod(step, GATES)
-            s, j = divmod(tile_index, TILES)
+            tile_index, gate, s, j = place(step)
             for a in range(BLOCKS_PER_GATE):
                 nc.tensor.matmul(
                     out=gate_ps[step][:, a * P : (a + 1) * P],
-                    lhsT=rec_T[s][:, gate * BLOCKS_PER_GATE + a, j * P : (j + 1) * P],
+                    lhsT=rec_T[s][:, TENSOR_JOINED.index(gate) * BLOCKS_PER_GATE + a, j * P : (j + 1) * P],
                     rhs=ident_f32[:],
                     is_transpose=True,
                     start=False,
@@ -161,7 +204,7 @@ def tile_nodelstmcell_pa_t_kernel(tc, x_t, h, c, W_ih, W_hh, b_ih, b_hh, out_0, 
         def new_cell(tile_index):
             s, j = divmod(tile_index, TILES)
             if j == 0:
-                c_new[s] = work.tile([P, TILES * HID], F32, name="c_new", tag="c_new")
+                c_new[s] = results.tile([P, TILES * HID], F32, name="c_new", tag="c_new")
             nc.vector.tensor_tensor(
                 out=c_new[s][:, j * HID : (j + 1) * HID],
                 in0=acts[tile_index, GATE_F][:],
@@ -179,7 +222,7 @@ def tile_nodelstmcell_pa_t_kernel(tc, x_t, h, c, W_ih, W_hh, b_ih, b_hh, out_0, 
         def new_hidden(tile_index):
             s, j = divmod(tile_index, TILES)
             if j == 0:
-                h_new[s] = work.tile([P, TILES * HID], F32, name="h_new", tag="h_new")
+                h_new[s] = results.tile([P, TILES * HID], F32, name="h_new", tag="h_new")
             nc.vector.tensor_tensor(
                 out=h_new[s][:, j * HID : (j + 1) * HID],
                 in0=acts[tile_index, GATE_O][:],
@@ -226,6 +269,15 @@ def tile_nodelstmcell_pa_t_kernel(tc, x_t, h, c, W_ih, W_hh, b_ih, b_hh, out_0, 
         nc.vector.tensor_copy(out=bias_pair[:], in_=biasT_ps[:, 0 : 2 * BLOCKS])
         bias = const.tile([P, BLOCKS], F32)
         nc.vector.tensor_tensor(out=bias[:], in0=bias_pair[:, 0:BLOCKS], in1=bias_pair[:, BLOCKS : 2 * BLOCKS], op=ALU.add)
+        bias_spread = const.tile([P, len(VECTOR_JOINED) * HID], F32)
+        for index, gate in enumerate(VECTOR_JOINED):
+            spread_ps = psum.tile([P, HID], F32, tag="gate", bufs=3)
+            for a in range(BLOCKS_PER_GATE):
+                blk = gate * BLOCKS_PER_GATE + a
+                nc.tensor.transpose(
+                    spread_ps[:, a * P : (a + 1) * P], bias[:, blk : blk + 1].to_broadcast([P, P]), ident_f32[:]
+                )
+            nc.scalar.copy(out=bias_spread[:, index * HID : (index + 1) * HID], in_=spread_ps[:])
 
         for j in range(TILES):
             quantise_rows(0, j, transpose_rows(0, j))
@@ -238,7 +290,7 @@ def tile_nodelstmcell_pa_t_kernel(tc, x_t, h, c, W_ih, W_hh, b_ih, b_hh, out_0, 
                 "p (a n u) -> p a n u", a=BLOCKS_PER_GATE, u=WORD_HALVES
             )
             for half in range(2):
-                wT_ps = psum.tile([P, 2, WORD_HALVES, P], F32, tag="gate", bufs=4)
+                wT_ps = psum.tile([P, 2, WORD_HALVES, P], F32, tag="gate", bufs=3)
                 for a in range(2):
                     raw_words = w_hh_raw[gate][:, 2 * half + a, :].bitcast(F32)
                     for u in range(WORD_HALVES):
@@ -248,12 +300,12 @@ def tile_nodelstmcell_pa_t_kernel(tc, x_t, h, c, W_ih, W_hh, b_ih, b_hh, out_0, 
                 )
             cols = slice(gate * HID, (gate + 1) * HID)
             nc.vector.quantize_mx(out=w_codes[:, cols].bitcast(FP8X4), scales=w_scales[:, cols], in_=w_grouped[:])
-            for a in range(BLOCKS_PER_GATE):
-                recurrent_block(0, gate * BLOCKS_PER_GATE + a)
+        for local in range(len(TENSOR_JOINED) * BLOCKS_PER_GATE):
+            recurrent_block(0, local)
 
         w_ih_T = const.tile([P, X_PASSES, GATES * HID], BF16)
         for gate in range(GATES):
-            wT_ps = psum.tile([P, X_PASSES, BLOCKS_PER_GATE, P], BF16, tag="gate", bufs=4)
+            wT_ps = psum.tile([P, X_PASSES, BLOCKS_PER_GATE, P], BF16, tag="gate", bufs=3)
             for a in range(BLOCKS_PER_GATE):
                 for kc in range(X_PASSES):
                     nc.tensor.transpose(wT_ps[:, kc, a, :], w_ih_raw[gate][:, a, kc * P : (kc + 1) * P], ident_bf16[:])
@@ -265,9 +317,8 @@ def tile_nodelstmcell_pa_t_kernel(tc, x_t, h, c, W_ih, W_hh, b_ih, b_hh, out_0, 
             quantise_rows(1, j, transpose_rows(1, j))
 
         grouped_waiting = {}
-        for step in range(N_STEPS + HIDDEN_LAG):
-            tile_index, gate = divmod(step, GATES)
-            s, j = divmod(tile_index, TILES)
+        for step in range((N_TILES - 1) * GATES + HIDDEN_LAG + 1):
+            tile_index, gate, s, j = place(step)
             running = step < N_STEPS
 
             if running and gate == 0 and j == 0:
@@ -278,8 +329,15 @@ def tile_nodelstmcell_pa_t_kernel(tc, x_t, h, c, W_ih, W_hh, b_ih, b_hh, out_0, 
 
             if running:
                 input_pass(step, 0)
-            if 0 < step <= N_STEPS:
+            if 0 < step <= N_STEPS and (step - 1) % GATES in TENSOR_JOINED:
                 add_recurrent_and_activate(step - 1)
+            if running and gate == 0 and s + 2 < N_GROUPS:
+                grouped_waiting[j] = transpose_rows(s + 2, j)
+            if running:
+                input_pass(step, 1)
+            if running and gate in VECTOR_JOINED:
+                add_bias(step)
+                recurrent_rows(step)
 
             due = tile_due(step, KEEP_LAG)
             if due is not None:
@@ -297,12 +355,9 @@ def tile_nodelstmcell_pa_t_kernel(tc, x_t, h, c, W_ih, W_hh, b_ih, b_hh, out_0, 
             if due is not None:
                 new_hidden(due)
 
-            if running and s + 2 < N_GROUPS:
-                if gate == 0:
-                    grouped_waiting[j] = transpose_rows(s + 2, j)
-                if gate == 1:
-                    quantise_rows(s + 2, j, grouped_waiting[j])
-            if running:
-                input_pass(step, 1)
-            if running and s + 1 < N_GROUPS:
-                recurrent_block(s + 1, j * GATES + gate)
+            if running and gate in VECTOR_JOINED:
+                join_and_activate(step)
+            if running and gate in TENSOR_JOINED and s + 1 < N_GROUPS:
+                recurrent_block(s + 1, j * len(TENSOR_JOINED) + TENSOR_JOINED.index(gate))
+            if running and gate == GATES - 1 and s + 2 < N_GROUPS:
+                quantise_rows(s + 2, j, grouped_waiting[j])

@@ -22,18 +22,24 @@ N_TILES = N_GROUPS * TILES
 N_STEPS = N_TILES * GATES
 BLOCKS_PER_GATE = HID // P
 BLOCKS = GATES * BLOCKS_PER_GATE
-X_PASSES = IN_DIM // P
-WORD_HALVES = 2
+PAIR = 2
+H_WORDS = HID // PAIR
+X_WORDS = IN_DIM // PAIR
+H_HALVES = H_WORDS // P
 PACK = 4
 
-VECTOR_JOINED = (GATE_I, GATE_F)
-TENSOR_JOINED = (GATE_G, GATE_O)
+VECTOR_JOINED = (GATE_I,)
+TENSOR_JOINED = (GATE_F, GATE_G, GATE_O)
+REC_BLOCKS = len(TENSOR_JOINED) * BLOCKS_PER_GATE
 
-KEEP_LAG = GATE_F + 1
-WRITE_LAG = GATE_G + 1
-CELL_LAG = GATES + GATE_F
+ACT_LAG = 1
+JOIN_LAG = 1
+KEEP_LAG = GATE_F + ACT_LAG + 1
+WRITE_LAG = GATE_G + ACT_LAG + 1
+CELL_LAG = WRITE_LAG + 2
 TANH_LAG = CELL_LAG + 1
-HIDDEN_LAG = 2 * GATES + GATE_I
+HIDDEN_LAG = TANH_LAG + 2
+QUANTISE_LAG = 2
 
 FLOPS = 2 * BATCH * GATES * HID * (IN_DIM + HID)
 
@@ -44,32 +50,34 @@ def tile_nodelstmcell_pa_t_kernel(tc, x_t, h, c, W_ih, W_hh, b_ih, b_hh, out_0, 
     x_rows = x_t.rearrange("(s p j) k -> s p (j k)", p=P, j=TILES)
     h_rows = h.rearrange("(s p j) k -> s p (j k)", p=P, j=TILES)
     c_rows = c.rearrange("(s p j) n -> s p (j n)", p=P, j=TILES)
-    h_next_rows = out_0.rearrange("(s p j) n -> s p (j n)", p=P, j=TILES)
-    c_next_rows = out_1.rearrange("(s p j) n -> s p (j n)", p=P, j=TILES)
+    h_next_rows = out_0.rearrange("(s p j) n -> s j p n", p=P, j=TILES)
+    c_next_rows = out_1.rearrange("(s p j) n -> s j p n", p=P, j=TILES)
 
     with ExitStack() as stack:
         const = stack.enter_context(tc.tile_pool(name="const", bufs=1))
         setup = stack.enter_context(tc.tile_pool(name="setup", bufs=4))
         rows = stack.enter_context(tc.tile_pool(name="rows", bufs=3))
-        operands = stack.enter_context(tc.tile_pool(name="operands", bufs=2))
+        operands = stack.enter_context(tc.tile_pool(name="operands", bufs=3))
         work = stack.enter_context(tc.tile_pool(name="work", bufs=3))
-        results = stack.enter_context(tc.tile_pool(name="results", bufs=2))
         psum = stack.enter_context(tc.psum_pool(name="psum", bufs=1))
         stack.enter_context(tc.manual_schedule())
 
         x_in, h_in, c_in = {}, {}, {}
         x_T, h_codes, h_scales = {}, {}, {}
+        h_grouped = {}
         rec_T = {}
         gate_ps = {}
         rec_ps = {}
         acts = {}
-        tanh_c = {}
-        c_new, h_new = {}, {}
+        c_new, tanh_c = {}, {}
 
         def place(step):
             tile_index, gate = divmod(step, GATES)
             s, j = divmod(tile_index, TILES)
             return tile_index, gate, s, j
+
+        def squash(gate):
+            return ACT.Tanh if gate == GATE_G else ACT.Sigmoid
 
         def load_rows(s):
             h_in[s] = rows.tile([P, TILES * HID], BF16, name="h_in", tag="h_in")
@@ -81,52 +89,46 @@ def tile_nodelstmcell_pa_t_kernel(tc, x_t, h, c, W_ih, W_hh, b_ih, b_hh, out_0, 
             c_in[s] = rows.tile([P, TILES * HID], BF16, name="c_in", tag="c_in")
             nc.sync.dma_start(out=c_in[s][:], in_=c_rows[s])
 
-        def transpose_rows(s, j):
+        def transpose_rows(tile_index):
+            s, j = divmod(tile_index, TILES)
             if j == 0:
-                h_codes[s] = operands.tile([P, GROUP_ROWS], U32, name="h_codes", tag="h_codes", bufs=3, align_bytes=64)
-                h_scales[s] = operands.tile([P, GROUP_ROWS], U8, name="h_scales", tag="h_scales", bufs=3, align_bytes=64)
-                x_T[s] = operands.tile([P, TILES, X_PASSES, P], BF16, name="x_T", tag="x_T", bufs=3)
+                h_codes[s] = operands.tile([P, GROUP_ROWS], U32, name="h_codes", tag="h_codes", align_bytes=64)
+                h_scales[s] = operands.tile([P, GROUP_ROWS], U8, name="h_scales", tag="h_scales", align_bytes=64)
+                x_T[s] = operands.tile([P, TILES, PAIR, P], BF16, name="x_T", tag="x_T")
+            words_ps = psum.tile([P, H_WORDS + X_WORDS], F32, tag="words")
             h_words = h_in[s][:].bitcast(F32)
-            hT_ps = psum.tile([P, WORD_HALVES, P], F32, tag="hT")
-            for u in range(WORD_HALVES):
-                first = (j * WORD_HALVES + u) * P
-                nc.tensor.transpose(hT_ps[:, u, :], h_words[:, first : first + P], ident_f32[:])
-            h_grouped = work.tile([P, P * PACK], BF16, tag="h_grouped", align_bytes=64)
+            for u in range(H_HALVES):
+                first = j * H_WORDS + u * P
+                nc.tensor.transpose(words_ps[:, u * P : (u + 1) * P], h_words[:, first : first + P], ident_f32[:])
+            x_words = x_in[s][:].bitcast(F32)
+            nc.tensor.transpose(words_ps[:, H_WORDS:], x_words[:, j * X_WORDS : (j + 1) * X_WORDS], ident_f32[:])
+            h_grouped[tile_index] = work.tile([P, P * PACK], BF16, name="h_grouped", tag="h_grouped", align_bytes=64)
             nc.scalar.copy(
-                out=h_grouped[:].bitcast(F32).rearrange("p (r u) -> p r u", u=WORD_HALVES),
-                in_=hT_ps[:].rearrange("p u r -> p r u"),
+                out=h_grouped[tile_index][:].bitcast(F32).rearrange("p (r u) -> p r u", u=H_HALVES),
+                in_=words_ps[:, 0:H_WORDS].rearrange("p (u r) -> p r u", u=H_HALVES),
             )
-            xT_ps = psum.tile([P, X_PASSES, P], BF16, tag="xT")
-            for kc in range(X_PASSES):
-                first = j * IN_DIM + kc * P
-                nc.tensor.transpose(xT_ps[:, kc, :], x_in[s][:, first : first + P], ident_bf16[:])
-            nc.scalar.copy(out=x_T[s][:, j, :, :], in_=xT_ps[:])
-            return h_grouped
+            nc.scalar.copy(
+                out=x_T[s][:, j, :, :],
+                in_=words_ps[:, H_WORDS:].bitcast(BF16).rearrange("p (r e) -> p e r", e=PAIR),
+            )
 
-        def quantise_rows(s, j, h_grouped):
+        def quantise_rows(tile_index):
+            s, j = divmod(tile_index, TILES)
             cols = slice(j * P, (j + 1) * P)
             nc.vector.quantize_mx(
-                out=h_codes[s][:, cols].bitcast(FP8X4), scales=h_scales[s][:, cols], in_=h_grouped[:]
+                out=h_codes[s][:, cols].bitcast(FP8X4), scales=h_scales[s][:, cols], in_=h_grouped[tile_index][:]
             )
 
-        def input_pass(step, kc):
+        def input_pass(step, e):
             tile_index, gate, s, j = place(step)
-            if kc == 0:
-                gate_ps[step] = psum.tile([P, HID], F32, name="gate_ps", tag="gate", bufs=3)
+            if e == 0:
+                gate_ps[step] = psum.tile([P, HID], F32, name="gate_ps", tag="gate", bufs=4)
             nc.tensor.matmul(
                 out=gate_ps[step][:],
-                lhsT=x_T[s][:, j, kc, :],
-                rhs=w_ih_T[:, kc, gate * HID : (gate + 1) * HID],
-                start=(kc == 0),
-                stop=(kc == X_PASSES - 1 and gate in VECTOR_JOINED),
-            )
-
-        def add_bias(step):
-            tile_index, gate, s, j = place(step)
-            acts[tile_index, gate] = work.tile([P, HID], F32, name="act%d" % gate, tag="act%d" % gate)
-            spread = VECTOR_JOINED.index(gate) * HID
-            nc.vector.tensor_tensor(
-                out=acts[tile_index, gate][:], in0=gate_ps[step][:], in1=bias_spread[:, spread : spread + HID], op=ALU.add
+                lhsT=x_T[s][:, j, e, :],
+                rhs=w_ih_T[:, e, gate * HID : (gate + 1) * HID],
+                start=(e == 0),
+                stop=(e == PAIR - 1 and gate in VECTOR_JOINED),
             )
 
         def recurrent_rows(step):
@@ -142,17 +144,27 @@ def tile_nodelstmcell_pa_t_kernel(tc, x_t, h, c, W_ih, W_hh, b_ih, b_hh, out_0, 
                 stop=True,
             )
 
-        def join_and_activate(step):
+        def add_bias(step):
+            tile_index, gate, s, j = place(step)
+            acts[tile_index, gate] = work.tile([P, HID], F32, name="act%d" % gate, tag="act%d" % gate)
+            first = VECTOR_JOINED.index(gate) * HID
+            nc.vector.tensor_tensor(
+                out=acts[tile_index, gate][:], in0=gate_ps[step][:], in1=bias_spread[:, first : first + HID], op=ALU.add
+            )
+
+        def join(step):
             tile_index, gate, s, j = place(step)
             total = acts[tile_index, gate]
             nc.vector.tensor_tensor(out=total[:], in0=rec_ps[step][:], in1=total[:], op=ALU.add)
-            nc.scalar.activation(out=total[:], in_=total[:], func=(ACT.Tanh if gate == GATE_G else ACT.Sigmoid))
+
+        def activate_joined(step):
+            tile_index, gate, s, j = place(step)
+            total = acts[tile_index, gate]
+            nc.scalar.activation(out=total[:], in_=total[:], func=squash(gate))
 
         def recurrent_block(s, local):
             if local == 0:
-                rec_T[s] = operands.tile(
-                    [P, len(TENSOR_JOINED) * BLOCKS_PER_GATE, GROUP_ROWS], F32, name="rec_T", tag="rec_T"
-                )
+                rec_T[s] = operands.tile([P, REC_BLOCKS, GROUP_ROWS], F32, name="rec_T", tag="rec_T", bufs=2)
             blk = TENSOR_JOINED[local // BLOCKS_PER_GATE] * BLOCKS_PER_GATE + local % BLOCKS_PER_GATE
             cols = slice(blk * P, (blk + 1) * P)
             recT_ps = psum.tile([P, GROUP_ROWS], F32, tag="rec", bufs=3)
@@ -165,16 +177,16 @@ def tile_nodelstmcell_pa_t_kernel(tc, x_t, h, c, W_ih, W_hh, b_ih, b_hh, out_0, 
                 start=True,
                 stop=True,
             )
-            if local % 2 == 0:
-                nc.scalar.activation(
-                    out=rec_T[s][:, local, :], in_=recT_ps[:], func=ACT.Identity, bias=bias[:, blk : blk + 1]
-                )
-            else:
+            if local % 3 == 2:
                 nc.vector.tensor_scalar(
                     out=rec_T[s][:, local, :], in0=recT_ps[:], scalar1=bias[:, blk : blk + 1], scalar2=None, op0=ALU.add
                 )
+            else:
+                nc.scalar.activation(
+                    out=rec_T[s][:, local, :], in_=recT_ps[:], func=ACT.Identity, bias=bias[:, blk : blk + 1]
+                )
 
-        def add_recurrent_and_activate(step):
+        def add_recurrent(step):
             tile_index, gate, s, j = place(step)
             for a in range(BLOCKS_PER_GATE):
                 nc.tensor.matmul(
@@ -185,12 +197,11 @@ def tile_nodelstmcell_pa_t_kernel(tc, x_t, h, c, W_ih, W_hh, b_ih, b_hh, out_0, 
                     start=False,
                     stop=(a == BLOCKS_PER_GATE - 1),
                 )
+
+        def activate_from_psum(step):
+            tile_index, gate, s, j = place(step)
             acts[tile_index, gate] = work.tile([P, HID], F32, name="act%d" % gate, tag="act%d" % gate)
-            nc.scalar.activation(
-                out=acts[tile_index, gate][:],
-                in_=gate_ps[step][:],
-                func=(ACT.Tanh if gate == GATE_G else ACT.Sigmoid),
-            )
+            nc.scalar.activation(out=acts[tile_index, gate][:], in_=gate_ps[step][:], func=squash(gate))
 
         def keep_old_cell(tile_index):
             s, j = divmod(tile_index, TILES)
@@ -203,34 +214,23 @@ def tile_nodelstmcell_pa_t_kernel(tc, x_t, h, c, W_ih, W_hh, b_ih, b_hh, out_0, 
 
         def new_cell(tile_index):
             s, j = divmod(tile_index, TILES)
-            if j == 0:
-                c_new[s] = results.tile([P, TILES * HID], F32, name="c_new", tag="c_new")
+            c_new[tile_index] = work.tile([P, HID], F32, name="c_new", tag="c_new")
             nc.vector.tensor_tensor(
-                out=c_new[s][:, j * HID : (j + 1) * HID],
-                in0=acts[tile_index, GATE_F][:],
-                in1=acts[tile_index, GATE_I][:],
-                op=ALU.add,
+                out=c_new[tile_index][:], in0=acts[tile_index, GATE_F][:], in1=acts[tile_index, GATE_I][:], op=ALU.add
             )
-            if j == TILES - 1:
-                nc.sync.dma_start(out=c_next_rows[s], in_=c_new[s][:])
+            nc.sync.dma_start(out=c_next_rows[s, j], in_=c_new[tile_index][:])
 
         def tanh_of_new_cell(tile_index):
-            s, j = divmod(tile_index, TILES)
             tanh_c[tile_index] = work.tile([P, HID], F32, name="tanh_c", tag="tanh_c")
-            nc.scalar.activation(out=tanh_c[tile_index][:], in_=c_new[s][:, j * HID : (j + 1) * HID], func=ACT.Tanh)
+            nc.scalar.activation(out=tanh_c[tile_index][:], in_=c_new[tile_index][:], func=ACT.Tanh)
 
         def new_hidden(tile_index):
             s, j = divmod(tile_index, TILES)
-            if j == 0:
-                h_new[s] = results.tile([P, TILES * HID], F32, name="h_new", tag="h_new")
+            h_new = work.tile([P, HID], F32, tag="h_new")
             nc.vector.tensor_tensor(
-                out=h_new[s][:, j * HID : (j + 1) * HID],
-                in0=acts[tile_index, GATE_O][:],
-                in1=tanh_c[tile_index][:],
-                op=ALU.mult,
+                out=h_new[:], in0=acts[tile_index, GATE_O][:], in1=tanh_c[tile_index][:], op=ALU.mult
             )
-            if j == TILES - 1:
-                nc.sync.dma_start(out=h_next_rows[s], in_=h_new[s][:])
+            nc.sync.dma_start(out=h_next_rows[s, j], in_=h_new[:])
 
         def tile_due(step, lag):
             tile_index, rest = divmod(step - lag, GATES)
@@ -243,17 +243,14 @@ def tile_nodelstmcell_pa_t_kernel(tc, x_t, h, c, W_ih, W_hh, b_ih, b_hh, out_0, 
         load_rows(0)
         w_hh_raw, w_ih_raw = [], []
         for gate in range(GATES):
-            raw = setup.tile([P, BLOCKS_PER_GATE, HID], BF16, name="w_hh_raw", tag="w_hh_raw")
+            w_hh_raw.append(setup.tile([P, BLOCKS_PER_GATE, HID], BF16, name="w_hh_raw", tag="w_hh_raw"))
             nc.sync.dma_start(
-                out=raw[:], in_=W_hh[gate * HID : (gate + 1) * HID, :].rearrange("(a p) k -> p a k", p=P)
+                out=w_hh_raw[gate][:], in_=W_hh[gate * HID : (gate + 1) * HID, :].rearrange("(a p) k -> p a k", p=P)
             )
-            w_hh_raw.append(raw)
-        for gate in range(GATES):
-            raw = setup.tile([P, BLOCKS_PER_GATE, IN_DIM], BF16, name="w_ih_raw", tag="w_ih_raw")
+            w_ih_raw.append(setup.tile([P, BLOCKS_PER_GATE, IN_DIM], BF16, name="w_ih_raw", tag="w_ih_raw"))
             nc.sync.dma_start(
-                out=raw[:], in_=W_ih[gate * HID : (gate + 1) * HID, :].rearrange("(a p) k -> p a k", p=P)
+                out=w_ih_raw[gate][:], in_=W_ih[gate * HID : (gate + 1) * HID, :].rearrange("(a p) k -> p a k", p=P)
             )
-            w_ih_raw.append(raw)
         load_rows(1)
         load_cell(0)
         load_rows(2)
@@ -263,7 +260,7 @@ def tile_nodelstmcell_pa_t_kernel(tc, x_t, h, c, W_ih, W_hh, b_ih, b_hh, out_0, 
         ident_bf16 = const.tile([P, P], BF16)
         make_identity(nc, ident_bf16[:])
 
-        biasT_ps = psum.tile([P, P], BF16, tag="xT")
+        biasT_ps = psum.tile([P, P], BF16, tag="words")
         nc.tensor.transpose(biasT_ps[:], bias_rows[:], ident_bf16[:])
         bias_pair = const.tile([P, 2 * BLOCKS], F32)
         nc.vector.tensor_copy(out=bias_pair[:], in_=biasT_ps[:, 0 : 2 * BLOCKS])
@@ -271,7 +268,7 @@ def tile_nodelstmcell_pa_t_kernel(tc, x_t, h, c, W_ih, W_hh, b_ih, b_hh, out_0, 
         nc.vector.tensor_tensor(out=bias[:], in0=bias_pair[:, 0:BLOCKS], in1=bias_pair[:, BLOCKS : 2 * BLOCKS], op=ALU.add)
         bias_spread = const.tile([P, len(VECTOR_JOINED) * HID], F32)
         for index, gate in enumerate(VECTOR_JOINED):
-            spread_ps = psum.tile([P, HID], F32, tag="gate", bufs=3)
+            spread_ps = psum.tile([P, HID], F32, tag="gate", bufs=4)
             for a in range(BLOCKS_PER_GATE):
                 blk = gate * BLOCKS_PER_GATE + a
                 nc.tensor.transpose(
@@ -279,44 +276,45 @@ def tile_nodelstmcell_pa_t_kernel(tc, x_t, h, c, W_ih, W_hh, b_ih, b_hh, out_0, 
                 )
             nc.scalar.copy(out=bias_spread[:, index * HID : (index + 1) * HID], in_=spread_ps[:])
 
-        for j in range(TILES):
-            quantise_rows(0, j, transpose_rows(0, j))
+        for tile_index in range(TILES):
+            transpose_rows(tile_index)
+            quantise_rows(tile_index)
 
         w_codes = const.tile([P, GATES * HID], U32, align_bytes=64)
         w_scales = const.tile([P, GATES * HID], U8, align_bytes=64)
+        w_ih_T = const.tile([P, PAIR, GATES * HID], BF16)
+
+        def first_group_blocks(gate):
+            if gate in TENSOR_JOINED:
+                for a in range(BLOCKS_PER_GATE):
+                    recurrent_block(0, TENSOR_JOINED.index(gate) * BLOCKS_PER_GATE + a)
+
         for gate in range(GATES):
+            cols = slice(gate * HID, (gate + 1) * HID)
             w_grouped = setup.tile([P, HID * PACK], BF16, tag="w_grouped", bufs=2, align_bytes=64)
             grouped_words = w_grouped[:].bitcast(F32).rearrange(
-                "p (a n u) -> p a n u", a=BLOCKS_PER_GATE, u=WORD_HALVES
+                "p (a n u) -> p a n u", a=BLOCKS_PER_GATE, u=H_HALVES
             )
             for half in range(2):
-                wT_ps = psum.tile([P, 2, WORD_HALVES, P], F32, tag="gate", bufs=3)
+                wT_ps = psum.tile([P, 2, H_HALVES, P], F32, tag="gate", bufs=4)
                 for a in range(2):
                     raw_words = w_hh_raw[gate][:, 2 * half + a, :].bitcast(F32)
-                    for u in range(WORD_HALVES):
+                    for u in range(H_HALVES):
                         nc.tensor.transpose(wT_ps[:, a, u, :], raw_words[:, u * P : (u + 1) * P], ident_f32[:])
-                nc.scalar.copy(
+                nc.vector.tensor_copy(
                     out=grouped_words[:, 2 * half : 2 * half + 2, :, :], in_=wT_ps[:].rearrange("p a u n -> p a n u")
                 )
-            cols = slice(gate * HID, (gate + 1) * HID)
             nc.vector.quantize_mx(out=w_codes[:, cols].bitcast(FP8X4), scales=w_scales[:, cols], in_=w_grouped[:])
-        for local in range(len(TENSOR_JOINED) * BLOCKS_PER_GATE):
-            recurrent_block(0, local)
-
-        w_ih_T = const.tile([P, X_PASSES, GATES * HID], BF16)
-        for gate in range(GATES):
-            wT_ps = psum.tile([P, X_PASSES, BLOCKS_PER_GATE, P], BF16, tag="gate", bufs=3)
+            wT_ps = psum.tile([P, HID], F32, tag="gate", bufs=4)
             for a in range(BLOCKS_PER_GATE):
-                for kc in range(X_PASSES):
-                    nc.tensor.transpose(wT_ps[:, kc, a, :], w_ih_raw[gate][:, a, kc * P : (kc + 1) * P], ident_bf16[:])
-            nc.scalar.copy(
-                out=w_ih_T[:, :, gate * HID : (gate + 1) * HID], in_=wT_ps[:].rearrange("p kc a n -> p kc (a n)")
-            )
+                nc.tensor.transpose(wT_ps[:, a * P : (a + 1) * P], w_ih_raw[gate][:, a, :].bitcast(F32), ident_f32[:])
+            nc.scalar.copy(out=w_ih_T[:, :, cols], in_=wT_ps[:].bitcast(BF16).rearrange("p (n e) -> p e n", e=PAIR))
+            first_group_blocks(gate - 1)
+        for tile_index in range(TILES, 2 * TILES):
+            transpose_rows(tile_index)
+            quantise_rows(tile_index)
+        first_group_blocks(GATES - 1)
 
-        for j in range(TILES):
-            quantise_rows(1, j, transpose_rows(1, j))
-
-        grouped_waiting = {}
         for step in range((N_TILES - 1) * GATES + HIDDEN_LAG + 1):
             tile_index, gate, s, j = place(step)
             running = step < N_STEPS
@@ -327,17 +325,27 @@ def tile_nodelstmcell_pa_t_kernel(tc, x_t, h, c, W_ih, W_hh, b_ih, b_hh, out_0, 
                 if s + 1 < N_GROUPS:
                     load_cell(s + 1)
 
+            started = step - ACT_LAG
+            finish_on_tensor = 0 <= started < N_STEPS and started % GATES in TENSOR_JOINED
+            rows_ahead = tile_index + 2 * TILES
             if running:
                 input_pass(step, 0)
-            if 0 < step <= N_STEPS and (step - 1) % GATES in TENSOR_JOINED:
-                add_recurrent_and_activate(step - 1)
-            if running and gate == 0 and s + 2 < N_GROUPS:
-                grouped_waiting[j] = transpose_rows(s + 2, j)
+            if finish_on_tensor:
+                add_recurrent(started)
+                activate_from_psum(started)
+            if running and gate == 0 and rows_ahead < N_TILES:
+                transpose_rows(rows_ahead)
             if running:
                 input_pass(step, 1)
             if running and gate in VECTOR_JOINED:
-                add_bias(step)
                 recurrent_rows(step)
+                add_bias(step)
+            if running and gate in TENSOR_JOINED and s + 1 < N_GROUPS:
+                recurrent_block(s + 1, j * len(TENSOR_JOINED) + TENSOR_JOINED.index(gate))
+            if 0 <= step - JOIN_LAG < N_STEPS and (step - JOIN_LAG) % GATES in VECTOR_JOINED:
+                join(step - JOIN_LAG)
+            if 0 <= step - JOIN_LAG - 1 < N_STEPS and (step - JOIN_LAG - 1) % GATES in VECTOR_JOINED:
+                activate_joined(step - JOIN_LAG - 1)
 
             due = tile_due(step, KEEP_LAG)
             if due is not None:
@@ -354,10 +362,6 @@ def tile_nodelstmcell_pa_t_kernel(tc, x_t, h, c, W_ih, W_hh, b_ih, b_hh, out_0, 
             due = tile_due(step, HIDDEN_LAG)
             if due is not None:
                 new_hidden(due)
-
-            if running and gate in VECTOR_JOINED:
-                join_and_activate(step)
-            if running and gate in TENSOR_JOINED and s + 1 < N_GROUPS:
-                recurrent_block(s + 1, j * len(TENSOR_JOINED) + TENSOR_JOINED.index(gate))
-            if running and gate == GATES - 1 and s + 2 < N_GROUPS:
-                quantise_rows(s + 2, j, grouped_waiting[j])
+            due = tile_due(step, QUANTISE_LAG)
+            if due is not None and due + 2 * TILES < N_TILES:
+                quantise_rows(due + 2 * TILES)

@@ -22,24 +22,13 @@ N_TILES = N_GROUPS * TILES
 N_STEPS = N_TILES * GATES
 BLOCKS_PER_GATE = HID // P
 BLOCKS = GATES * BLOCKS_PER_GATE
+BLOCKS_PER_TILE = BLOCKS // TILES
 PAIR = 2
 H_WORDS = HID // PAIR
 X_WORDS = IN_DIM // PAIR
 H_HALVES = H_WORDS // P
 PACK = 4
-
-VECTOR_JOINED = (GATE_I,)
-TENSOR_JOINED = (GATE_F, GATE_G, GATE_O)
-REC_BLOCKS = len(TENSOR_JOINED) * BLOCKS_PER_GATE
-
-ACT_LAG = 1
-JOIN_LAG = 1
-KEEP_LAG = GATE_F + ACT_LAG + 1
-WRITE_LAG = GATE_G + ACT_LAG + 1
-CELL_LAG = WRITE_LAG + 2
-TANH_LAG = CELL_LAG + 1
-HIDDEN_LAG = TANH_LAG + 2
-QUANTISE_LAG = 2
+ROWS_AHEAD = 2 * TILES
 
 FLOPS = 2 * BATCH * GATES * HID * (IN_DIM + HID)
 
@@ -59,7 +48,7 @@ def tile_nodelstmcell_pa_t_kernel(tc, x_t, h, c, W_ih, W_hh, b_ih, b_hh, out_0, 
         rows = stack.enter_context(tc.tile_pool(name="rows", bufs=3))
         operands = stack.enter_context(tc.tile_pool(name="operands", bufs=3))
         work = stack.enter_context(tc.tile_pool(name="work", bufs=3))
-        psum = stack.enter_context(tc.psum_pool(name="psum", bufs=1))
+        psum = stack.enter_context(tc.psum_pool(name="psum", bufs=4))
         stack.enter_context(tc.manual_schedule())
 
         x_in, h_in, c_in = {}, {}, {}
@@ -67,7 +56,6 @@ def tile_nodelstmcell_pa_t_kernel(tc, x_t, h, c, W_ih, W_hh, b_ih, b_hh, out_0, 
         h_grouped = {}
         rec_T = {}
         gate_ps = {}
-        rec_ps = {}
         acts = {}
         c_new, tanh_c = {}, {}
 
@@ -75,9 +63,6 @@ def tile_nodelstmcell_pa_t_kernel(tc, x_t, h, c, W_ih, W_hh, b_ih, b_hh, out_0, 
             tile_index, gate = divmod(step, GATES)
             s, j = divmod(tile_index, TILES)
             return tile_index, gate, s, j
-
-        def squash(gate):
-            return ACT.Tanh if gate == GATE_G else ACT.Sigmoid
 
         def load_rows(s):
             h_in[s] = rows.tile([P, TILES * HID], BF16, name="h_in", tag="h_in")
@@ -95,7 +80,7 @@ def tile_nodelstmcell_pa_t_kernel(tc, x_t, h, c, W_ih, W_hh, b_ih, b_hh, out_0, 
                 h_codes[s] = operands.tile([P, GROUP_ROWS], U32, name="h_codes", tag="h_codes", align_bytes=64)
                 h_scales[s] = operands.tile([P, GROUP_ROWS], U8, name="h_scales", tag="h_scales", align_bytes=64)
                 x_T[s] = operands.tile([P, TILES, PAIR, P], BF16, name="x_T", tag="x_T")
-            words_ps = psum.tile([P, H_WORDS + X_WORDS], F32, tag="words")
+            words_ps = psum.tile([P, H_WORDS + X_WORDS], F32, tag="copied_out")
             h_words = h_in[s][:].bitcast(F32)
             for u in range(H_HALVES):
                 first = j * H_WORDS + u * P
@@ -107,7 +92,7 @@ def tile_nodelstmcell_pa_t_kernel(tc, x_t, h, c, W_ih, W_hh, b_ih, b_hh, out_0, 
                 out=h_grouped[tile_index][:].bitcast(F32).rearrange("p (r u) -> p r u", u=H_HALVES),
                 in_=words_ps[:, 0:H_WORDS].rearrange("p (u r) -> p r u", u=H_HALVES),
             )
-            nc.scalar.copy(
+            nc.vector.tensor_copy(
                 out=x_T[s][:, j, :, :],
                 in_=words_ps[:, H_WORDS:].bitcast(BF16).rearrange("p (r e) -> p e r", e=PAIR),
             )
@@ -119,55 +104,11 @@ def tile_nodelstmcell_pa_t_kernel(tc, x_t, h, c, W_ih, W_hh, b_ih, b_hh, out_0, 
                 out=h_codes[s][:, cols].bitcast(FP8X4), scales=h_scales[s][:, cols], in_=h_grouped[tile_index][:]
             )
 
-        def input_pass(step, e):
-            tile_index, gate, s, j = place(step)
-            if e == 0:
-                gate_ps[step] = psum.tile([P, HID], F32, name="gate_ps", tag="gate", bufs=4)
-            nc.tensor.matmul(
-                out=gate_ps[step][:],
-                lhsT=x_T[s][:, j, e, :],
-                rhs=w_ih_T[:, e, gate * HID : (gate + 1) * HID],
-                start=(e == 0),
-                stop=(e == PAIR - 1 and gate in VECTOR_JOINED),
-            )
-
-        def recurrent_rows(step):
-            tile_index, gate, s, j = place(step)
-            rec_ps[step] = psum.tile([P, HID], F32, name="rec_ps", tag="rec", bufs=3)
-            nc.tensor.matmul_mx(
-                out=rec_ps[step][:],
-                lhsT=h_codes[s][:, j * P : (j + 1) * P].bitcast(FP8X4),
-                lhsT_scale=h_scales[s][:, j * P : (j + 1) * P],
-                rhs=w_codes[:, gate * HID : (gate + 1) * HID].bitcast(FP8X4),
-                rhs_scale=w_scales[:, gate * HID : (gate + 1) * HID],
-                start=True,
-                stop=True,
-            )
-
-        def add_bias(step):
-            tile_index, gate, s, j = place(step)
-            acts[tile_index, gate] = work.tile([P, HID], F32, name="act%d" % gate, tag="act%d" % gate)
-            first = VECTOR_JOINED.index(gate) * HID
-            nc.vector.tensor_tensor(
-                out=acts[tile_index, gate][:], in0=gate_ps[step][:], in1=bias_spread[:, first : first + HID], op=ALU.add
-            )
-
-        def join(step):
-            tile_index, gate, s, j = place(step)
-            total = acts[tile_index, gate]
-            nc.vector.tensor_tensor(out=total[:], in0=rec_ps[step][:], in1=total[:], op=ALU.add)
-
-        def activate_joined(step):
-            tile_index, gate, s, j = place(step)
-            total = acts[tile_index, gate]
-            nc.scalar.activation(out=total[:], in_=total[:], func=squash(gate))
-
-        def recurrent_block(s, local):
-            if local == 0:
-                rec_T[s] = operands.tile([P, REC_BLOCKS, GROUP_ROWS], F32, name="rec_T", tag="rec_T", bufs=2)
-            blk = TENSOR_JOINED[local // BLOCKS_PER_GATE] * BLOCKS_PER_GATE + local % BLOCKS_PER_GATE
+        def recurrent_block(s, blk, on_scalar):
+            if blk == 0:
+                rec_T[s] = operands.tile([P, BLOCKS, GROUP_ROWS], F32, name="rec_T", tag="rec_T", bufs=2)
             cols = slice(blk * P, (blk + 1) * P)
-            recT_ps = psum.tile([P, GROUP_ROWS], F32, tag="rec", bufs=3)
+            recT_ps = psum.tile([P, GROUP_ROWS], F32, tag="copied_out")
             nc.tensor.matmul_mx(
                 out=recT_ps[:],
                 lhsT=w_codes[:, cols].bitcast(FP8X4),
@@ -177,31 +118,47 @@ def tile_nodelstmcell_pa_t_kernel(tc, x_t, h, c, W_ih, W_hh, b_ih, b_hh, out_0, 
                 start=True,
                 stop=True,
             )
-            if local % 3 == 2:
-                nc.vector.tensor_scalar(
-                    out=rec_T[s][:, local, :], in0=recT_ps[:], scalar1=bias[:, blk : blk + 1], scalar2=None, op0=ALU.add
+            if on_scalar:
+                nc.scalar.activation(
+                    out=rec_T[s][:, blk, :], in_=recT_ps[:], func=ACT.Identity, bias=bias[:, blk : blk + 1]
                 )
             else:
-                nc.scalar.activation(
-                    out=rec_T[s][:, local, :], in_=recT_ps[:], func=ACT.Identity, bias=bias[:, blk : blk + 1]
+                nc.vector.tensor_scalar(
+                    out=rec_T[s][:, blk, :], in0=recT_ps[:], scalar1=bias[:, blk : blk + 1], scalar2=None, op0=ALU.add
                 )
 
-        def add_recurrent(step):
+        def input_pass(step, e):
             tile_index, gate, s, j = place(step)
-            for a in range(BLOCKS_PER_GATE):
+            if e == 0:
+                gate_ps[step] = psum.tile([P, HID], F32, name="gate_ps", tag="gate")
+            nc.tensor.matmul(
+                out=gate_ps[step][:],
+                lhsT=x_T[s][:, j, e, :],
+                rhs=w_ih_T[:, e, gate * HID : (gate + 1) * HID],
+                start=(e == 0),
+                stop=False,
+            )
+
+        def add_recurrent(step, half):
+            tile_index, gate, s, j = place(step)
+            for a in range(PAIR * half, PAIR * half + PAIR):
                 nc.tensor.matmul(
                     out=gate_ps[step][:, a * P : (a + 1) * P],
-                    lhsT=rec_T[s][:, TENSOR_JOINED.index(gate) * BLOCKS_PER_GATE + a, j * P : (j + 1) * P],
+                    lhsT=rec_T[s][:, gate * BLOCKS_PER_GATE + a, j * P : (j + 1) * P],
                     rhs=ident_f32[:],
                     is_transpose=True,
                     start=False,
                     stop=(a == BLOCKS_PER_GATE - 1),
                 )
 
-        def activate_from_psum(step):
+        def activate(step):
             tile_index, gate, s, j = place(step)
             acts[tile_index, gate] = work.tile([P, HID], F32, name="act%d" % gate, tag="act%d" % gate)
-            nc.scalar.activation(out=acts[tile_index, gate][:], in_=gate_ps[step][:], func=squash(gate))
+            nc.scalar.activation(
+                out=acts[tile_index, gate][:],
+                in_=gate_ps[step][:],
+                func=(ACT.Tanh if gate == GATE_G else ACT.Sigmoid),
+            )
 
         def keep_old_cell(tile_index):
             s, j = divmod(tile_index, TILES)
@@ -232,10 +189,6 @@ def tile_nodelstmcell_pa_t_kernel(tc, x_t, h, c, W_ih, W_hh, b_ih, b_hh, out_0, 
             )
             nc.sync.dma_start(out=h_next_rows[s, j], in_=h_new[:])
 
-        def tile_due(step, lag):
-            tile_index, rest = divmod(step - lag, GATES)
-            return tile_index if rest == 0 and 0 <= tile_index < N_TILES else None
-
         bias_rows = const.tile([P, P], BF16)
         nc.vector.memset(bias_rows[:], 0.0)
         nc.sync.dma_start(out=bias_rows[0:BLOCKS, :], in_=b_ih.rearrange("(b n) -> b n", n=P))
@@ -260,21 +213,12 @@ def tile_nodelstmcell_pa_t_kernel(tc, x_t, h, c, W_ih, W_hh, b_ih, b_hh, out_0, 
         ident_bf16 = const.tile([P, P], BF16)
         make_identity(nc, ident_bf16[:])
 
-        biasT_ps = psum.tile([P, P], BF16, tag="words")
+        biasT_ps = psum.tile([P, P], BF16, tag="copied_out")
         nc.tensor.transpose(biasT_ps[:], bias_rows[:], ident_bf16[:])
         bias_pair = const.tile([P, 2 * BLOCKS], F32)
         nc.vector.tensor_copy(out=bias_pair[:], in_=biasT_ps[:, 0 : 2 * BLOCKS])
         bias = const.tile([P, BLOCKS], F32)
         nc.vector.tensor_tensor(out=bias[:], in0=bias_pair[:, 0:BLOCKS], in1=bias_pair[:, BLOCKS : 2 * BLOCKS], op=ALU.add)
-        bias_spread = const.tile([P, len(VECTOR_JOINED) * HID], F32)
-        for index, gate in enumerate(VECTOR_JOINED):
-            spread_ps = psum.tile([P, HID], F32, tag="gate", bufs=4)
-            for a in range(BLOCKS_PER_GATE):
-                blk = gate * BLOCKS_PER_GATE + a
-                nc.tensor.transpose(
-                    spread_ps[:, a * P : (a + 1) * P], bias[:, blk : blk + 1].to_broadcast([P, P]), ident_f32[:]
-                )
-            nc.scalar.copy(out=bias_spread[:, index * HID : (index + 1) * HID], in_=spread_ps[:])
 
         for tile_index in range(TILES):
             transpose_rows(tile_index)
@@ -285,9 +229,8 @@ def tile_nodelstmcell_pa_t_kernel(tc, x_t, h, c, W_ih, W_hh, b_ih, b_hh, out_0, 
         w_ih_T = const.tile([P, PAIR, GATES * HID], BF16)
 
         def first_group_blocks(gate):
-            if gate in TENSOR_JOINED:
-                for a in range(BLOCKS_PER_GATE):
-                    recurrent_block(0, TENSOR_JOINED.index(gate) * BLOCKS_PER_GATE + a)
+            for a in range(BLOCKS_PER_GATE):
+                recurrent_block(0, gate * BLOCKS_PER_GATE + a, on_scalar=(a % 2 == 1))
 
         for gate in range(GATES):
             cols = slice(gate * HID, (gate + 1) * HID)
@@ -296,72 +239,62 @@ def tile_nodelstmcell_pa_t_kernel(tc, x_t, h, c, W_ih, W_hh, b_ih, b_hh, out_0, 
                 "p (a n u) -> p a n u", a=BLOCKS_PER_GATE, u=H_HALVES
             )
             for half in range(2):
-                wT_ps = psum.tile([P, 2, H_HALVES, P], F32, tag="gate", bufs=4)
+                wT_ps = psum.tile([P, 2, H_HALVES, P], F32, tag="gate")
                 for a in range(2):
                     raw_words = w_hh_raw[gate][:, 2 * half + a, :].bitcast(F32)
                     for u in range(H_HALVES):
                         nc.tensor.transpose(wT_ps[:, a, u, :], raw_words[:, u * P : (u + 1) * P], ident_f32[:])
-                nc.vector.tensor_copy(
+                copy_out = nc.vector.tensor_copy if half == 0 else nc.scalar.copy
+                copy_out(
                     out=grouped_words[:, 2 * half : 2 * half + 2, :, :], in_=wT_ps[:].rearrange("p a u n -> p a n u")
                 )
             nc.vector.quantize_mx(out=w_codes[:, cols].bitcast(FP8X4), scales=w_scales[:, cols], in_=w_grouped[:])
-            wT_ps = psum.tile([P, HID], F32, tag="gate", bufs=4)
+            wT_ps = psum.tile([P, HID], F32, tag="gate")
             for a in range(BLOCKS_PER_GATE):
                 nc.tensor.transpose(wT_ps[:, a * P : (a + 1) * P], w_ih_raw[gate][:, a, :].bitcast(F32), ident_f32[:])
             nc.scalar.copy(out=w_ih_T[:, :, cols], in_=wT_ps[:].bitcast(BF16).rearrange("p (n e) -> p e n", e=PAIR))
-            first_group_blocks(gate - 1)
-        for tile_index in range(TILES, 2 * TILES):
+            if gate > 0:
+                first_group_blocks(gate - 1)
+        for tile_index in range(TILES, ROWS_AHEAD):
             transpose_rows(tile_index)
             quantise_rows(tile_index)
         first_group_blocks(GATES - 1)
 
-        for step in range((N_TILES - 1) * GATES + HIDDEN_LAG + 1):
-            tile_index, gate, s, j = place(step)
-            running = step < N_STEPS
-
-            if running and gate == 0 and j == 0:
+        for turn in range(N_TILES + 2):
+            s, j = divmod(turn, TILES)
+            running = turn < N_TILES
+            if running and j == 0:
                 if s + 3 < N_GROUPS:
                     load_rows(s + 3)
                 if s + 1 < N_GROUPS:
                     load_cell(s + 1)
 
-            started = step - ACT_LAG
-            finish_on_tensor = 0 <= started < N_STEPS and started % GATES in TENSOR_JOINED
-            rows_ahead = tile_index + 2 * TILES
-            if running:
-                input_pass(step, 0)
-            if finish_on_tensor:
-                add_recurrent(started)
-                activate_from_psum(started)
-            if running and gate == 0 and rows_ahead < N_TILES:
-                transpose_rows(rows_ahead)
-            if running:
-                input_pass(step, 1)
-            if running and gate in VECTOR_JOINED:
-                recurrent_rows(step)
-                add_bias(step)
-            if running and gate in TENSOR_JOINED and s + 1 < N_GROUPS:
-                recurrent_block(s + 1, j * len(TENSOR_JOINED) + TENSOR_JOINED.index(gate))
-            if 0 <= step - JOIN_LAG < N_STEPS and (step - JOIN_LAG) % GATES in VECTOR_JOINED:
-                join(step - JOIN_LAG)
-            if 0 <= step - JOIN_LAG - 1 < N_STEPS and (step - JOIN_LAG - 1) % GATES in VECTOR_JOINED:
-                activate_joined(step - JOIN_LAG - 1)
+            for gate in range(GATES):
+                step = turn * GATES + gate
+                before = step - 1
+                for e in range(PAIR):
+                    if running:
+                        input_pass(step, e)
+                    if 0 <= before < N_STEPS:
+                        add_recurrent(before, e)
+                if 0 <= before < N_STEPS:
+                    activate(before)
 
-            due = tile_due(step, KEEP_LAG)
-            if due is not None:
-                keep_old_cell(due)
-            due = tile_due(step, WRITE_LAG)
-            if due is not None:
-                write_candidate(due)
-            due = tile_due(step, CELL_LAG)
-            if due is not None:
-                new_cell(due)
-            due = tile_due(step, TANH_LAG)
-            if due is not None:
-                tanh_of_new_cell(due)
-            due = tile_due(step, HIDDEN_LAG)
-            if due is not None:
-                new_hidden(due)
-            due = tile_due(step, QUANTISE_LAG)
-            if due is not None and due + 2 * TILES < N_TILES:
-                quantise_rows(due + 2 * TILES)
+                if gate == GATE_I:
+                    if turn + ROWS_AHEAD < N_TILES:
+                        transpose_rows(turn + ROWS_AHEAD)
+                    if running and s + 1 < N_GROUPS:
+                        for b in range(BLOCKS_PER_TILE):
+                            recurrent_block(s + 1, j * BLOCKS_PER_TILE + b, on_scalar=(b == 1))
+                    if 0 <= turn - 1 < N_TILES:
+                        keep_old_cell(turn - 1)
+                        write_candidate(turn - 1)
+                    if 0 <= turn - 2 < N_TILES:
+                        tanh_of_new_cell(turn - 2)
+
+            if 0 <= turn - 1 < N_TILES:
+                new_cell(turn - 1)
+            if 0 <= turn - 2 < N_TILES:
+                new_hidden(turn - 2)
+            if turn + ROWS_AHEAD < N_TILES:
+                quantise_rows(turn + ROWS_AHEAD)

@@ -22,7 +22,9 @@ N_TILES = N_GROUPS * TILES
 N_STEPS = N_TILES * GATES
 BLOCKS_PER_GATE = HID // P
 BLOCKS = GATES * BLOCKS_PER_GATE
-BLOCKS_PER_TILE = BLOCKS // TILES
+REC_GATES = (GATE_F, GATE_G, GATE_O)
+REC_BLOCKS = len(REC_GATES) * BLOCKS_PER_GATE
+REC_BLOCKS_PER_TILE = REC_BLOCKS // TILES
 PAIR = 2
 H_WORDS = HID // PAIR
 X_WORDS = IN_DIM // PAIR
@@ -56,6 +58,7 @@ def tile_nodelstmcell_pa_t_kernel(tc, x_t, h, c, W_ih, W_hh, b_ih, b_hh, out_0, 
         h_grouped = {}
         rec_T = {}
         gate_ps = {}
+        rec_ps = {}
         acts = {}
         c_new, tanh_c = {}, {}
 
@@ -92,7 +95,7 @@ def tile_nodelstmcell_pa_t_kernel(tc, x_t, h, c, W_ih, W_hh, b_ih, b_hh, out_0, 
                 out=h_grouped[tile_index][:].bitcast(F32).rearrange("p (r u) -> p r u", u=H_HALVES),
                 in_=words_ps[:, 0:H_WORDS].rearrange("p (u r) -> p r u", u=H_HALVES),
             )
-            nc.vector.tensor_copy(
+            nc.scalar.copy(
                 out=x_T[s][:, j, :, :],
                 in_=words_ps[:, H_WORDS:].bitcast(BF16).rearrange("p (r e) -> p e r", e=PAIR),
             )
@@ -104,9 +107,10 @@ def tile_nodelstmcell_pa_t_kernel(tc, x_t, h, c, W_ih, W_hh, b_ih, b_hh, out_0, 
                 out=h_codes[s][:, cols].bitcast(FP8X4), scales=h_scales[s][:, cols], in_=h_grouped[tile_index][:]
             )
 
-        def recurrent_block(s, blk, on_scalar):
-            if blk == 0:
-                rec_T[s] = operands.tile([P, BLOCKS, GROUP_ROWS], F32, name="rec_T", tag="rec_T", bufs=2)
+        def recurrent_block(s, local, on_scalar):
+            if local == 0:
+                rec_T[s] = operands.tile([P, REC_BLOCKS, GROUP_ROWS], F32, name="rec_T", tag="rec_T", bufs=2)
+            blk = REC_GATES[0] * BLOCKS_PER_GATE + local
             cols = slice(blk * P, (blk + 1) * P)
             recT_ps = psum.tile([P, GROUP_ROWS], F32, tag="copied_out")
             nc.tensor.matmul_mx(
@@ -120,12 +124,35 @@ def tile_nodelstmcell_pa_t_kernel(tc, x_t, h, c, W_ih, W_hh, b_ih, b_hh, out_0, 
             )
             if on_scalar:
                 nc.scalar.activation(
-                    out=rec_T[s][:, blk, :], in_=recT_ps[:], func=ACT.Identity, bias=bias[:, blk : blk + 1]
+                    out=rec_T[s][:, local, :], in_=recT_ps[:], func=ACT.Identity, bias=bias[:, blk : blk + 1]
                 )
             else:
                 nc.vector.tensor_scalar(
-                    out=rec_T[s][:, blk, :], in0=recT_ps[:], scalar1=bias[:, blk : blk + 1], scalar2=None, op0=ALU.add
+                    out=rec_T[s][:, local, :], in0=recT_ps[:], scalar1=bias[:, blk : blk + 1], scalar2=None, op0=ALU.add
                 )
+
+        def recurrent_rows(tile_index):
+            s, j = divmod(tile_index, TILES)
+            rec_ps[tile_index] = psum.tile([P, HID], F32, name="rec_ps", tag="copied_out")
+            nc.tensor.matmul_mx(
+                out=rec_ps[tile_index][:],
+                lhsT=h_codes[s][:, j * P : (j + 1) * P].bitcast(FP8X4),
+                lhsT_scale=h_scales[s][:, j * P : (j + 1) * P],
+                rhs=w_codes[:, GATE_I * HID : (GATE_I + 1) * HID].bitcast(FP8X4),
+                rhs_scale=w_scales[:, GATE_I * HID : (GATE_I + 1) * HID],
+                start=True,
+                stop=True,
+            )
+
+        def add_bias(tile_index):
+            acts[tile_index, GATE_I] = work.tile([P, HID], F32, name="act%d" % GATE_I, tag="act%d" % GATE_I)
+            nc.vector.tensor_tensor(
+                out=acts[tile_index, GATE_I][:], in0=gate_ps[tile_index * GATES + GATE_I][:], in1=bias_spread[:], op=ALU.add
+            )
+
+        def add_recurrent_rows(tile_index):
+            total = acts[tile_index, GATE_I]
+            nc.vector.tensor_tensor(out=total[:], in0=rec_ps[tile_index][:], in1=total[:], op=ALU.add)
 
         def input_pass(step, e):
             tile_index, gate, s, j = place(step)
@@ -136,7 +163,7 @@ def tile_nodelstmcell_pa_t_kernel(tc, x_t, h, c, W_ih, W_hh, b_ih, b_hh, out_0, 
                 lhsT=x_T[s][:, j, e, :],
                 rhs=w_ih_T[:, e, gate * HID : (gate + 1) * HID],
                 start=(e == 0),
-                stop=False,
+                stop=(e == PAIR - 1 and gate == GATE_I),
             )
 
         def add_recurrent(step, half):
@@ -144,7 +171,7 @@ def tile_nodelstmcell_pa_t_kernel(tc, x_t, h, c, W_ih, W_hh, b_ih, b_hh, out_0, 
             for a in range(PAIR * half, PAIR * half + PAIR):
                 nc.tensor.matmul(
                     out=gate_ps[step][:, a * P : (a + 1) * P],
-                    lhsT=rec_T[s][:, gate * BLOCKS_PER_GATE + a, j * P : (j + 1) * P],
+                    lhsT=rec_T[s][:, REC_GATES.index(gate) * BLOCKS_PER_GATE + a, j * P : (j + 1) * P],
                     rhs=ident_f32[:],
                     is_transpose=True,
                     start=False,
@@ -153,12 +180,16 @@ def tile_nodelstmcell_pa_t_kernel(tc, x_t, h, c, W_ih, W_hh, b_ih, b_hh, out_0, 
 
         def activate(step):
             tile_index, gate, s, j = place(step)
-            acts[tile_index, gate] = work.tile([P, HID], F32, name="act%d" % gate, tag="act%d" % gate)
-            nc.scalar.activation(
-                out=acts[tile_index, gate][:],
-                in_=gate_ps[step][:],
-                func=(ACT.Tanh if gate == GATE_G else ACT.Sigmoid),
-            )
+            if gate == GATE_I:
+                total = acts[tile_index, gate]
+                nc.scalar.activation(out=total[:], in_=total[:], func=ACT.Sigmoid)
+            else:
+                acts[tile_index, gate] = work.tile([P, HID], F32, name="act%d" % gate, tag="act%d" % gate)
+                nc.scalar.activation(
+                    out=acts[tile_index, gate][:],
+                    in_=gate_ps[step][:],
+                    func=(ACT.Tanh if gate == GATE_G else ACT.Sigmoid),
+                )
 
         def keep_old_cell(tile_index):
             s, j = divmod(tile_index, TILES)
@@ -219,6 +250,14 @@ def tile_nodelstmcell_pa_t_kernel(tc, x_t, h, c, W_ih, W_hh, b_ih, b_hh, out_0, 
         nc.vector.tensor_copy(out=bias_pair[:], in_=biasT_ps[:, 0 : 2 * BLOCKS])
         bias = const.tile([P, BLOCKS], F32)
         nc.vector.tensor_tensor(out=bias[:], in0=bias_pair[:, 0:BLOCKS], in1=bias_pair[:, BLOCKS : 2 * BLOCKS], op=ALU.add)
+        bias_spread = const.tile([P, HID], F32)
+        spread_ps = psum.tile([P, HID], F32, tag="gate")
+        for a in range(BLOCKS_PER_GATE):
+            blk = GATE_I * BLOCKS_PER_GATE + a
+            nc.tensor.transpose(
+                spread_ps[:, a * P : (a + 1) * P], bias[:, blk : blk + 1].to_broadcast([P, P]), ident_f32[:]
+            )
+        nc.scalar.copy(out=bias_spread[:], in_=spread_ps[:])
 
         for tile_index in range(TILES):
             transpose_rows(tile_index)
@@ -229,8 +268,9 @@ def tile_nodelstmcell_pa_t_kernel(tc, x_t, h, c, W_ih, W_hh, b_ih, b_hh, out_0, 
         w_ih_T = const.tile([P, PAIR, GATES * HID], BF16)
 
         def first_group_blocks(gate):
-            for a in range(BLOCKS_PER_GATE):
-                recurrent_block(0, gate * BLOCKS_PER_GATE + a, on_scalar=(a % 2 == 1))
+            if gate in REC_GATES:
+                for a in range(BLOCKS_PER_GATE):
+                    recurrent_block(0, REC_GATES.index(gate) * BLOCKS_PER_GATE + a, on_scalar=(a % 2 == 1))
 
         for gate in range(GATES):
             cols = slice(gate * HID, (gate + 1) * HID)
@@ -272,25 +312,35 @@ def tile_nodelstmcell_pa_t_kernel(tc, x_t, h, c, W_ih, W_hh, b_ih, b_hh, out_0, 
             for gate in range(GATES):
                 step = turn * GATES + gate
                 before = step - 1
-                for e in range(PAIR):
-                    if running:
-                        input_pass(step, e)
-                    if 0 <= before < N_STEPS:
-                        add_recurrent(before, e)
-                if 0 <= before < N_STEPS:
-                    activate(before)
+                finish = 0 <= before < N_STEPS
+                finish_by_transposes = finish and before % GATES in REC_GATES
 
-                if gate == GATE_I:
-                    if turn + ROWS_AHEAD < N_TILES:
-                        transpose_rows(turn + ROWS_AHEAD)
+                if running:
+                    input_pass(step, 0)
+                if finish_by_transposes:
+                    add_recurrent(before, 0)
+                if gate == GATE_F:
+                    if running:
+                        recurrent_rows(turn)
+                        add_recurrent_rows(turn)
                     if running and s + 1 < N_GROUPS:
-                        for b in range(BLOCKS_PER_TILE):
-                            recurrent_block(s + 1, j * BLOCKS_PER_TILE + b, on_scalar=(b == 1))
+                        for b in range(REC_BLOCKS_PER_TILE):
+                            recurrent_block(s + 1, j * REC_BLOCKS_PER_TILE + b, on_scalar=(b == 0))
                     if 0 <= turn - 1 < N_TILES:
                         keep_old_cell(turn - 1)
                         write_candidate(turn - 1)
                     if 0 <= turn - 2 < N_TILES:
                         tanh_of_new_cell(turn - 2)
+                if running:
+                    input_pass(step, 1)
+                if finish_by_transposes:
+                    add_recurrent(before, 1)
+                if gate == GATE_F and turn + ROWS_AHEAD < N_TILES:
+                    transpose_rows(turn + ROWS_AHEAD)
+                if finish:
+                    activate(before)
+                if gate == GATE_I and running:
+                    add_bias(turn)
 
             if 0 <= turn - 1 < N_TILES:
                 new_cell(turn - 1)

from contextlib import ExitStack

import concourse.mybir as mybir
from concourse.masks import make_identity

F32 = mybir.dt.float32
BF16 = mybir.dt.bfloat16
U32 = mybir.dt.uint32
U8 = mybir.dt.uint8
FP8X4 = mybir.dt.float8_e4m3fn_x4
ACT = mybir.ActivationFunctionType
ALU = mybir.AluOpType

P = 128
BATCH, IN_DIM, HID = 4096, 256, 512
GATES = 4
GATE_I, GATE_F, GATE_G, GATE_O = 0, 1, 2, 3
TILES = 4
GROUP_ROWS = TILES * P
N_GROUPS = BATCH // GROUP_ROWS
N_TILES = N_GROUPS * TILES
N_STEPS = N_TILES * GATES
BLOCKS_PER_GATE = HID // P
BLOCKS = GATES * BLOCKS_PER_GATE
REC_GATES = (GATE_F, GATE_G, GATE_O)
REC_BLOCKS = len(REC_GATES) * BLOCKS_PER_GATE
REC_BLOCKS_PER_TILE = REC_BLOCKS // TILES
PAIR = 2
H_WORDS = HID // PAIR
X_WORDS = IN_DIM // PAIR
H_HALVES = H_WORDS // P
PACK = 4
ROWS_AHEAD = 2 * TILES

FLOPS = 2 * BATCH * GATES * HID * (IN_DIM + HID)


def tile_nodelstmcell_pa_t_kernel(tc, x_t, h, c, W_ih, W_hh, b_ih, b_hh, out_0, out_1):
    nc = tc.nc

    x_rows = x_t.rearrange("(s p j) k -> s p (j k)", p=P, j=TILES)
    h_rows = h.rearrange("(s p j) k -> s p (j k)", p=P, j=TILES)
    c_rows = c.rearrange("(s p j) n -> s p (j n)", p=P, j=TILES)
    h_next_rows = out_0.rearrange("(s p j) n -> s j p n", p=P, j=TILES)
    c_next_rows = out_1.rearrange("(s p j) n -> s j p n", p=P, j=TILES)

    with ExitStack() as stack:
        const = stack.enter_context(tc.tile_pool(name="const", bufs=1))
        setup = stack.enter_context(tc.tile_pool(name="setup", bufs=4))
        rows = stack.enter_context(tc.tile_pool(name="rows", bufs=3))
        operands = stack.enter_context(tc.tile_pool(name="operands", bufs=3))
        work = stack.enter_context(tc.tile_pool(name="work", bufs=3))
        psum = stack.enter_context(tc.psum_pool(name="psum", bufs=4))
        stack.enter_context(tc.manual_schedule())

        x_in, h_in, c_in = {}, {}, {}
        x_T, h_codes, h_scales = {}, {}, {}
        h_grouped = {}
        rec_T = {}
        gate_ps = {}
        rec_ps = {}
        acts = {}
        c_new, tanh_c = {}, {}

        def place(step):
            tile_index, gate = divmod(step, GATES)
            s, j = divmod(tile_index, TILES)
            return tile_index, gate, s, j

        def load_rows(s):
            h_in[s] = rows.tile([P, TILES * HID], BF16, name="h_in", tag="h_in")
            nc.sync.dma_start(out=h_in[s][:], in_=h_rows[s])
            x_in[s] = rows.tile([P, TILES * IN_DIM], BF16, name="x_in", tag="x_in")
            nc.sync.dma_start(out=x_in[s][:], in_=x_rows[s])

        def load_cell(s):
            c_in[s] = rows.tile([P, TILES * HID], BF16, name="c_in", tag="c_in")
            nc.sync.dma_start(out=c_in[s][:], in_=c_rows[s])

        def transpose_rows(tile_index):
            s, j = divmod(tile_index, TILES)
            if j == 0:
                h_codes[s] = operands.tile([P, GROUP_ROWS], U32, name="h_codes", tag="h_codes", align_bytes=64)
                h_scales[s] = operands.tile([P, GROUP_ROWS], U8, name="h_scales", tag="h_scales", align_bytes=64)
                x_T[s] = operands.tile([P, TILES, PAIR, P], BF16, name="x_T", tag="x_T")
            words_ps = psum.tile([P, H_WORDS + X_WORDS], F32, tag="copied_out")
            h_words = h_in[s][:].bitcast(F32)
            for u in range(H_HALVES):
                first = j * H_WORDS + u * P
                nc.tensor.transpose(words_ps[:, u * P : (u + 1) * P], h_words[:, first : first + P], ident_f32[:])
            x_words = x_in[s][:].bitcast(F32)
            nc.tensor.transpose(words_ps[:, H_WORDS:], x_words[:, j * X_WORDS : (j + 1) * X_WORDS], ident_f32[:])
            h_grouped[tile_index] = work.tile([P, P * PACK], BF16, name="h_grouped", tag="h_grouped", align_bytes=64)
            nc.scalar.copy(
                out=h_grouped[tile_index][:].bitcast(F32).rearrange("p (r u) -> p r u", u=H_HALVES),
                in_=words_ps[:, 0:H_WORDS].rearrange("p (u r) -> p r u", u=H_HALVES),
            )
            nc.scalar.copy(
                out=x_T[s][:, j, :, :],
                in_=words_ps[:, H_WORDS:].bitcast(BF16).rearrange("p (r e) -> p e r", e=PAIR),
            )

        def quantise_rows(tile_index):
            s, j = divmod(tile_index, TILES)
            cols = slice(j * P, (j + 1) * P)
            nc.vector.quantize_mx(
                out=h_codes[s][:, cols].bitcast(FP8X4), scales=h_scales[s][:, cols], in_=h_grouped[tile_index][:]
            )

        def recurrent_block(s, local, on_scalar):
            if local == 0:
                rec_T[s] = operands.tile([P, REC_BLOCKS, GROUP_ROWS], F32, name="rec_T", tag="rec_T", bufs=2)
            blk = REC_GATES[0] * BLOCKS_PER_GATE + local
            cols = slice(blk * P, (blk + 1) * P)
            recT_ps = psum.tile([P, GROUP_ROWS], F32, tag="copied_out")
            nc.tensor.matmul_mx(
                out=recT_ps[:],
                lhsT=w_codes[:, cols].bitcast(FP8X4),
                lhsT_scale=w_scales[:, cols],
                rhs=h_codes[s][:].bitcast(FP8X4),
                rhs_scale=h_scales[s][:],
                start=True,
                stop=True,
            )
            if on_scalar:
                nc.scalar.activation(
                    out=rec_T[s][:, local, :], in_=recT_ps[:], func=ACT.Identity, bias=bias[:, blk : blk + 1]
                )
            else:
                nc.vector.tensor_scalar(
                    out=rec_T[s][:, local, :], in0=recT_ps[:], scalar1=bias[:, blk : blk + 1], scalar2=None, op0=ALU.add
                )

        def recurrent_rows(tile_index):
            s, j = divmod(tile_index, TILES)
            rec_ps[tile_index] = psum.tile([P, HID], F32, name="rec_ps", tag="copied_out")
            nc.tensor.matmul_mx(
                out=rec_ps[tile_index][:],
                lhsT=h_codes[s][:, j * P : (j + 1) * P].bitcast(FP8X4),
                lhsT_scale=h_scales[s][:, j * P : (j + 1) * P],
                rhs=w_codes[:, GATE_I * HID : (GATE_I + 1) * HID].bitcast(FP8X4),
                rhs_scale=w_scales[:, GATE_I * HID : (GATE_I + 1) * HID],
                start=True,
                stop=True,
            )

        def add_bias(tile_index):
            acts[tile_index, GATE_I] = work.tile([P, HID], F32, name="act%d" % GATE_I, tag="act%d" % GATE_I)
            nc.vector.tensor_tensor(
                out=acts[tile_index, GATE_I][:], in0=gate_ps[tile_index * GATES + GATE_I][:], in1=bias_spread[:], op=ALU.add
            )

        def add_recurrent_rows(tile_index):
            total = acts[tile_index, GATE_I]
            nc.vector.tensor_tensor(out=total[:], in0=rec_ps[tile_index][:], in1=total[:], op=ALU.add)

        def input_pass(step, e):
            tile_index, gate, s, j = place(step)
            if e == 0:
                gate_ps[step] = psum.tile([P, HID], F32, name="gate_ps", tag="gate")
            nc.tensor.matmul(
                out=gate_ps[step][:],
                lhsT=x_T[s][:, j, e, :],
                rhs=w_ih_T[:, e, gate * HID : (gate + 1) * HID],
                start=(e == 0),
                stop=(e == PAIR - 1 and gate == GATE_I),
            )

        def add_recurrent(step, half):
            tile_index, gate, s, j = place(step)
            for a in range(PAIR * half, PAIR * half + PAIR):
                nc.tensor.matmul(
                    out=gate_ps[step][:, a * P : (a + 1) * P],
                    lhsT=rec_T[s][:, REC_GATES.index(gate) * BLOCKS_PER_GATE + a, j * P : (j + 1) * P],
                    rhs=ident_f32[:],
                    is_transpose=True,
                    start=False,
                    stop=(a == BLOCKS_PER_GATE - 1),
                )

        def activate(step):
            tile_index, gate, s, j = place(step)
            if gate == GATE_I:
                total = acts[tile_index, gate]
                nc.scalar.activation(out=total[:], in_=total[:], func=ACT.Sigmoid)
            else:
                acts[tile_index, gate] = work.tile([P, HID], F32, name="act%d" % gate, tag="act%d" % gate)
                nc.scalar.activation(
                    out=acts[tile_index, gate][:],
                    in_=gate_ps[step][:],
                    func=(ACT.Tanh if gate == GATE_G else ACT.Sigmoid),
                )

        def keep_old_cell(tile_index):
            s, j = divmod(tile_index, TILES)
            keep = acts[tile_index, GATE_F]
            nc.gpsimd.tensor_tensor(out=keep[:], in0=keep[:], in1=c_in[s][:, j * HID : (j + 1) * HID], op=ALU.mult)

        def write_candidate(tile_index):
            write = acts[tile_index, GATE_I]
            nc.gpsimd.tensor_tensor(out=write[:], in0=write[:], in1=acts[tile_index, GATE_G][:], op=ALU.mult)

        def new_cell(tile_index):
            s, j = divmod(tile_index, TILES)
            c_new[tile_index] = work.tile([P, HID], F32, name="c_new", tag="c_new")
            nc.vector.tensor_tensor(
                out=c_new[tile_index][:], in0=acts[tile_index, GATE_F][:], in1=acts[tile_index, GATE_I][:], op=ALU.add
            )
            nc.sync.dma_start(out=c_next_rows[s, j], in_=c_new[tile_index][:])

        def tanh_of_new_cell(tile_index):
            tanh_c[tile_index] = work.tile([P, HID], F32, name="tanh_c", tag="tanh_c")
            nc.scalar.activation(out=tanh_c[tile_index][:], in_=c_new[tile_index][:], func=ACT.Tanh)

        def new_hidden(tile_index):
            s, j = divmod(tile_index, TILES)
            h_new = work.tile([P, HID], F32, tag="h_new")
            nc.vector.tensor_tensor(
                out=h_new[:], in0=acts[tile_index, GATE_O][:], in1=tanh_c[tile_index][:], op=ALU.mult
            )
            nc.sync.dma_start(out=h_next_rows[s, j], in_=h_new[:])

        bias_rows = const.tile([P, P], BF16)
        nc.vector.memset(bias_rows[:], 0.0)
        nc.sync.dma_start(out=bias_rows[0:BLOCKS, :], in_=b_ih.rearrange("(b n) -> b n", n=P))
        nc.sync.dma_start(out=bias_rows[BLOCKS : 2 * BLOCKS, :], in_=b_hh.rearrange("(b n) -> b n", n=P))
        load_rows(0)
        w_hh_raw, w_ih_raw = [], []
        for gate in range(GATES):
            w_hh_raw.append(setup.tile([P, BLOCKS_PER_GATE, HID], BF16, name="w_hh_raw", tag="w_hh_raw"))
            nc.sync.dma_start(
                out=w_hh_raw[gate][:], in_=W_hh[gate * HID : (gate + 1) * HID, :].rearrange("(a p) k -> p a k", p=P)
            )
            w_ih_raw.append(setup.tile([P, BLOCKS_PER_GATE, IN_DIM], BF16, name="w_ih_raw", tag="w_ih_raw"))
            nc.sync.dma_start(
                out=w_ih_raw[gate][:], in_=W_ih[gate * HID : (gate + 1) * HID, :].rearrange("(a p) k -> p a k", p=P)
            )
        load_rows(1)
        load_cell(0)
        load_rows(2)

        ident_f32 = const.tile([P, P], F32)
        make_identity(nc, ident_f32[:])
        ident_bf16 = const.tile([P, P], BF16)
        make_identity(nc, ident_bf16[:])

        biasT_ps = psum.tile([P, P], BF16, tag="copied_out")
        nc.tensor.transpose(biasT_ps[:], bias_rows[:], ident_bf16[:])
        bias_pair = const.tile([P, 2 * BLOCKS], F32)
        nc.vector.tensor_copy(out=bias_pair[:], in_=biasT_ps[:, 0 : 2 * BLOCKS])
        bias = const.tile([P, BLOCKS], F32)
        nc.vector.tensor_tensor(out=bias[:], in0=bias_pair[:, 0:BLOCKS], in1=bias_pair[:, BLOCKS : 2 * BLOCKS], op=ALU.add)
        bias_spread = const.tile([P, HID], F32)
        spread_ps = psum.tile([P, HID], F32, tag="gate")
        for a in range(BLOCKS_PER_GATE):
            blk = GATE_I * BLOCKS_PER_GATE + a
            nc.tensor.transpose(
                spread_ps[:, a * P : (a + 1) * P], bias[:, blk : blk + 1].to_broadcast([P, P]), ident_f32[:]
            )
        nc.scalar.copy(out=bias_spread[:], in_=spread_ps[:])

        for tile_index in range(TILES):
            transpose_rows(tile_index)
            quantise_rows(tile_index)

        w_codes = const.tile([P, GATES * HID], U32, align_bytes=64)
        w_scales = const.tile([P, GATES * HID], U8, align_bytes=64)
        w_ih_T = const.tile([P, PAIR, GATES * HID], BF16)

        def first_group_blocks(gate):
            if gate in REC_GATES:
                for a in range(BLOCKS_PER_GATE):
                    recurrent_block(0, REC_GATES.index(gate) * BLOCKS_PER_GATE + a, on_scalar=(a % 2 == 1))

        for gate in range(GATES):
            cols = slice(gate * HID, (gate + 1) * HID)
            w_grouped = setup.tile([P, HID * PACK], BF16, tag="w_grouped", bufs=2, align_bytes=64)
            grouped_words = w_grouped[:].bitcast(F32).rearrange(
                "p (a n u) -> p a n u", a=BLOCKS_PER_GATE, u=H_HALVES
            )
            for half in range(2):
                wT_ps = psum.tile([P, 2, H_HALVES, P], F32, tag="gate")
                for a in range(2):
                    raw_words = w_hh_raw[gate][:, 2 * half + a, :].bitcast(F32)
                    for u in range(H_HALVES):
                        nc.tensor.transpose(wT_ps[:, a, u, :], raw_words[:, u * P : (u + 1) * P], ident_f32[:])
                copy_out = nc.vector.tensor_copy if half == 0 else nc.scalar.copy
                copy_out(
                    out=grouped_words[:, 2 * half : 2 * half + 2, :, :], in_=wT_ps[:].rearrange("p a u n -> p a n u")
                )
            nc.vector.quantize_mx(out=w_codes[:, cols].bitcast(FP8X4), scales=w_scales[:, cols], in_=w_grouped[:])
            wT_ps = psum.tile([P, HID], F32, tag="gate")
            for a in range(BLOCKS_PER_GATE):
                nc.tensor.transpose(wT_ps[:, a * P : (a + 1) * P], w_ih_raw[gate][:, a, :].bitcast(F32), ident_f32[:])
            nc.scalar.copy(out=w_ih_T[:, :, cols], in_=wT_ps[:].bitcast(BF16).rearrange("p (n e) -> p e n", e=PAIR))
            if gate > 0:
                first_group_blocks(gate - 1)
        for tile_index in range(TILES, ROWS_AHEAD):
            transpose_rows(tile_index)
            quantise_rows(tile_index)
        first_group_blocks(GATES - 1)

        for turn in range(N_TILES + 2):
            s, j = divmod(turn, TILES)
            running = turn < N_TILES
            if running and j == 0:
                if s + 3 < N_GROUPS:
                    load_rows(s + 3)
                if s + 1 < N_GROUPS:
                    load_cell(s + 1)

            for gate in range(GATES):
                step = turn * GATES + gate
                before = step - 1
                finish = 0 <= before < N_STEPS
                finish_by_transposes = finish and before % GATES in REC_GATES

                if running:
                    input_pass(step, 0)
                if finish_by_transposes:
                    add_recurrent(before, 0)
                if gate == GATE_F:
                    if running:
                        recurrent_rows(turn)
                        add_recurrent_rows(turn)
                    if running and s + 1 < N_GROUPS:
                        for b in range(REC_BLOCKS_PER_TILE):
                            recurrent_block(s + 1, j * REC_BLOCKS_PER_TILE + b, on_scalar=(b == 0))
                    if 0 <= turn - 1 < N_TILES:
                        keep_old_cell(turn - 1)
                        write_candidate(turn - 1)
                    if 0 <= turn - 2 < N_TILES:
                        tanh_of_new_cell(turn - 2)
                if running:
                    input_pass(step, 1)
                if finish_by_transposes:
                    add_recurrent(before, 1)
                if gate == GATE_F and turn + ROWS_AHEAD < N_TILES:
                    transpose_rows(turn + ROWS_AHEAD)
                if finish:
                    activate(before)
                if gate == GATE_I and running:
                    add_bias(turn)

            if 0 <= turn - 1 < N_TILES:
                new_cell(turn - 1)
            if 0 <= turn - 2 < N_TILES:
                new_hidden(turn - 2)
            if turn + ROWS_AHEAD < N_TILES:
                quantise_rows(turn + ROWS_AHEAD)
